import numpy as np
import ml_dtypes


def mxq(x, axis, fmt="e4m3"):
    dtype, down = {"e4m3": (ml_dtypes.float8_e4m3fn, 7), "e5m2": (ml_dtypes.float8_e5m2, 14)}[fmt]
    v = np.moveaxis(np.asarray(x, np.float32).astype(ml_dtypes.bfloat16).astype(np.float64), axis, -1)
    blocks = v.reshape(v.shape[:-1] + (-1, 32))
    amax = np.abs(blocks).max(-1, keepdims=True)
    byte = np.maximum(np.where(amax > 0, np.frexp(amax)[1] - 1 + 127, 0) - down, 1)
    scale = np.exp2(byte - 127.0)
    codes = (blocks / scale).astype(np.float32).astype(dtype).astype(np.float64)
    return np.moveaxis((codes * scale).reshape(v.shape), -1, axis)


WIDE = False


def mx_kscale(k):
    if not WIDE:
        return np.ones(k)
    levels = np.array([18, -18])
    if k % 512:
        return np.exp2(np.random.permutation(np.resize(levels, k // 32))).repeat(32)
    a = np.empty((k // 512, 16))
    for p in range(k // 512):
        a[p, :8] = np.random.permutation(np.resize(levels, 8))
        for g in range(8):
            far = levels[np.abs(levels - a[p, g]) >= 10]
            a[p, g + 8] = far[np.random.randint(len(far))]
    return np.exp2(a.ravel()).repeat(32)


BF16 = ml_dtypes.bfloat16


def bf(x):
    return np.asarray(x, np.float32).astype(BF16)


def f64(x):
    return np.asarray(x).astype(np.float64)


N, D, H = 1024, 128, 512
EPS = 1e-5


def adj(d1):
    eye = np.eye(d1.shape[0])
    return (1.0 / (d1 + EPS)) * (1.0 - eye) + eye


def inv_sqrt_deg(d1):
    return 1.0 / np.sqrt(np.sum(adj(d1), axis=1))


def norm_adj(d1):
    dinv = inv_sqrt_deg(d1)
    return dinv[:, None] * adj(d1) * dinv[None, :]


def draw_d1():
    c = np.random.uniform(0.5, 1.5, N)
    e = np.exp(0.7 * np.random.standard_normal((N, N)))
    d = 0.56 * D * 0.5 * (c[:, None] + c[None, :]) * e * (1.0 - np.eye(N))
    return bf(d)


def setup_inputs():
    u = mx_kscale(N)
    s = mx_kscale(N)
    v = mx_kscale(H)
    r = np.minimum(s, u)
    d1_t0 = draw_d1()
    d1_f = draw_d1()
    xt0 = bf(np.random.standard_normal((N, D)))
    xf = bf(np.random.standard_normal((N, D)))
    W_gt0 = bf(np.random.standard_normal((D, H)) / np.sqrt(D))
    W_gf = bf(np.random.standard_normal((D, H)) / np.sqrt(D))
    b_g = bf(np.random.standard_normal(H) * 0.1)
    g = bf(16.0 * np.random.standard_normal((N, H)) * np.exp2(np.random.randint(-6, 1, (N, 1))) / u[:, None] * v[None, :])
    dinv_t = inv_sqrt_deg(f64(d1_t0))
    z = norm_adj(f64(d1_t0)) @ (f64(xt0) @ f64(W_gt0)) + norm_adj(f64(d1_f)) @ (f64(xf) @ f64(W_gf)) + f64(b_g)
    return {"d1_t": bf(f64(d1_t0) * s[None, :] / u[:, None]), "d1_f": d1_f,
            "xt": bf(f64(xt0) * r[:, None]), "xf": xf,
            "W_gt": bf(f64(W_gt0) / v[None, :]), "W_gf": W_gf, "b_g": b_g,
            "z": np.asarray(z, np.float32), "dinv_t": np.asarray(dinv_t, np.float32), "grad_out": g}


def reference(d1_t, d1_f, xt, xf, W_gt, W_gf, b_g, z, dinv_t, grad_out):
    di = f64(dinv_t)[:, None]
    a = adj(f64(d1_t))
    dz2 = f64(grad_out) * (f64(z) > 0.0) * di
    dh = mxq(a, 0, "e4m3").T @ mxq(dz2, 0, "e5m2")
    dz1 = dh * di
    dxt = mxq(dz1, 1, "e5m2") @ mxq(f64(W_gt), 1, "e4m3").T
    dW = mxq(f64(xt), 0, "e4m3").T @ mxq(dz1, 0, "e5m2")
    return dxt, dW

@@ -1,0 +1,375 @@
+from contextlib import ExitStack
+
+import concourse.mybir as mybir
+from concourse.masks import make_identity
+
+N, D, H = 1024, 128, 512
+EPS = 1e-5
+FLOPS = 2 * N * N * H + 2 * N * H * D + 2 * N * D * H
+BYTES = 2 * N * N + 2 * N * D + 2 * D * H + 4 * N * H + 4 * N + 2 * N * H + 4 * N * D + 4 * D * H
+
+F32 = mybir.dt.float32
+BF16 = mybir.dt.bfloat16
+U32 = mybir.dt.uint32
+U8 = mybir.dt.uint8
+E4M3 = mybir.dt.float8_e4m3fn_x4
+E5M2 = mybir.dt.float8_e5m2_x4
+ACT = mybir.ActivationFunctionType
+ALU = mybir.AluOpType
+
+P = 128
+PACK = 4
+PASS = P * PACK
+PASSES = N // PASS
+HUGE = 2.0 ** 120
+
+
+def tile_ensemblenet_pa_v_kernel(tc, d1_t, d1_f, xt, xf, W_gt, W_gf, b_g, z, dinv_t, grad_out, out_0, out_1):
+    nc = tc.nc
+    with ExitStack() as ctx:
+        sb = ctx.enter_context(tc.tile_pool(name="sb", bufs=1))
+        ps = ctx.enter_context(tc.psum_pool(name="ps", bufs=1))
+        ctx.enter_context(tc.manual_schedule())
+
+        def sbuf(name, width, dtype):
+            return sb.tile([P, width], dtype, name=name, align_bytes=64)
+
+        def bank(number, name):
+            return ps.tile([P, PASS], F32, name=name, tag="bank%d" % number)
+
+        pairs = [(g, c) for g in range(PASSES) for c in range(PASSES)]
+        dist = {(g, c, half): sbuf("dist%d%d%d" % (g, c, half), 2 * PASS, BF16) for g, c in pairs for half in range(2)}
+        root = {(g, c): sbuf("root%d%d" % (g, c), PACK * PASS, F32) for g, c in pairs}
+        adj = {(g, c): sbuf("adj%d%d" % (g, c), PACK * PASS, BF16) for g, c in pairs}
+        adj_codes = {(g, c): sbuf("adj_codes%d%d" % (g, c), PASS, U32) for g, c in pairs}
+        adj_scales = {(g, c): sbuf("adj_scales%d%d" % (g, c), PASS, U8) for g, c in pairs}
+        halves = [(g, half) for g in range(PASSES) for half in range(2)]
+        z_sb = {k: sbuf("z%d%d" % k, 2 * H, F32) for k in halves}
+        grad = {k: sbuf("grad%d%d" % k, 2 * H, BF16) for k in halves}
+        masked = {k: sbuf("masked%d%d" % k, 2 * H, BF16) for k in halves}
+        dz2_rows = [sbuf("dz2_rows%d" % g, PACK * H, BF16) for g in range(PASSES)]
+        dz2 = [sbuf("dz2_%d" % g, PACK * H, BF16) for g in range(PASSES)]
+        dz2_codes = [sbuf("dz2_codes%d" % g, H, U32) for g in range(PASSES)]
+        dz2_scales = [sbuf("dz2_scales%d" % g, H, U8) for g in range(PASSES)]
+        dz1_rows = [sbuf("dz1_rows%d" % c, PACK * H, BF16) for c in range(PASSES)]
+        dz1_by_node = [sbuf("dz1_by_node%d" % c, PACK * H, BF16) for c in range(PASSES)]
+        node_codes = [sbuf("node_codes%d" % c, H, U32) for c in range(PASSES)]
+        node_scales = [sbuf("node_scales%d" % c, H, U8) for c in range(PASSES)]
+        dz1_by_feat = {k: sbuf("dz1_by_feat%d%d" % k, 2 * H, BF16) for k in halves}
+        feat_codes = {k: sbuf("feat_codes%d%d" % k, 2 * P, U32) for k in halves}
+        feat_scales = {k: sbuf("feat_scales%d%d" % k, 2 * P, U8) for k in halves}
+        x_rows = sbuf("x_rows", PASSES * PACK * D, BF16)
+        x_packed = sbuf("x_packed", PASSES * PACK * D, BF16)
+        x_codes = sbuf("x_codes", PASSES * D, U32)
+        x_scales = sbuf("x_scales", PASSES * D, U8)
+        w_rows = sbuf("w_rows", H, BF16)
+        w_packed = sbuf("w_packed", PACK * D, BF16)
+        w_codes = sbuf("w_codes", (2 * PACK - 1) * D, U32)
+        w_scales = sbuf("w_scales", (2 * PACK - 1) * D, U8)
+        dinv = sbuf("dinv", PASSES * PACK, F32)
+        ident = sbuf("ident", P, F32)
+        loop_cap = sbuf("loop_cap", PASS, F32)
+        warm = sbuf("warm", 8, F32)
+        dx_sb = [sbuf("dx_sb%d" % c, PACK * D, F32) for c in range(PASSES)]
+        dw_sb = sbuf("dw_sb", H, F32)
+        dh, flipped, dx_ps, dw_ps = {}, {}, {}, {}
+
+        def rows_of(src, g, half):
+            return src[g * PASS:(g + 1) * PASS, :].rearrange("(p t) w -> p t w", t=PACK)[:, 2 * half:2 * half + 2, :]
+
+        def load_dist(g, c, half):
+            nc.sync.dma_start(out=dist[g, c, half][:].rearrange("p (t j) -> p t j", t=2),
+                              in_=rows_of(d1_t, g, half)[:, :, c * PASS:(c + 1) * PASS])
+
+        def load_z(g, half):
+            nc.sync.dma_start(out=z_sb[g, half][:].rearrange("p (t h) -> p t h", t=2), in_=rows_of(z, g, half))
+
+        def load_grad(g, half):
+            nc.sync.dma_start(out=grad[g, half][:].rearrange("p (t h) -> p t h", t=2), in_=rows_of(grad_out, g, half))
+
+        def load_x():
+            nc.sync.dma_start(out=x_rows[:].rearrange("p (c w) -> p c w", c=PASSES),
+                              in_=xt.rearrange("(c p s) d -> p c (s d)", c=PASSES, s=PACK))
+
+        def load_w():
+            nc.sync.dma_start(out=w_rows[:], in_=W_gt)
+
+        def constants():
+            nc.scalar.dma_start(out=dinv[:].rearrange("p (g t) -> p g t", g=PASSES),
+                                in_=dinv_t.rearrange("(g p t) -> p g t", g=PASSES, t=PACK))
+            nc.vector.memset(warm[:], 1.0)
+            nc.scalar.activation(out=warm[:, 0:1], in_=warm[:, 0:1], func=ACT.Abs_reciprocal_sqrt)
+            nc.vector.memset(loop_cap[:], HUGE)
+            nc.gpsimd.affine_select(out=loop_cap[:], in_=loop_cap[:], pattern=[[PACK, P], [1, 2], [-1, 2]],
+                                    compare_op=ALU.not_equal, fill=-1.0, base=0, channel_multiplier=-PACK)
+            make_identity(nc, ident[:])
+            nc.vector.memset(w_codes[:], 0)
+            nc.vector.memset(w_scales[:].bitcast(U32), 0)
+
+        def inverse_root(g, c, half):
+            nc.scalar.activation(out=root[g, c][:, half * 2 * PASS:(half + 1) * 2 * PASS].rearrange("p (j t) -> p j t", t=2),
+                                 in_=dist[g, c, half][:].rearrange("p (t j) -> p j t", t=2),
+                                 func=ACT.Abs_reciprocal_sqrt, bias=EPS)
+
+        def self_loops(g, half):
+            lines = root[g, g][:].rearrange("p (a m b q) -> p a b m q", a=2, b=2, q=PACK)[:, half, half]
+            nc.vector.tensor_tensor(out=lines, in0=lines, in1=loop_cap[:].rearrange("p (m q) -> p m q", q=PACK), op=ALU.min)
+
+        def square(engine, g, c, s):
+            src = root[g, c][:].rearrange("p (a m s t) -> p s m a t", a=2, s=PACK, t=2)[:, s]
+            dst = adj[g, c][:, s * PASS:(s + 1) * PASS].rearrange("p (m a t) -> p m a t", a=2, t=2)
+            if engine == "scalar":
+                nc.scalar.activation(out=dst, in_=src, func=ACT.Square)
+            else:
+                nc.vector.tensor_tensor(out=dst, in0=src, in1=src, op=ALU.mult)
+
+        def quantise(values, codes, scales, fmt, first, count):
+            nc.vector.quantize_mx(out=codes[:, first:first + count].bitcast(fmt), scales=scales[:, first:first + count],
+                                  in_=values)
+
+        def quantise_adj(g, c, s0, s1):
+            quantise(adj[g, c][:, s0 * PASS:s1 * PASS], adj_codes[g, c], adj_scales[g, c], E4M3, s0 * P, (s1 - s0) * P)
+
+        def interleave(dst, src):
+            nc.vector.tensor_copy(out=dst.rearrange("p (c i t) -> p c t i", i=4, t=PACK), in_=src)
+
+        def mask_grad(g, half):
+            nc.vector.scalar_tensor_tensor(out=masked[g, half][:], in0=z_sb[g, half][:], scalar=0.0, in1=grad[g, half][:],
+                                           op0=ALU.is_gt, op1=ALU.mult)
+
+        def scale_grad(g, half):
+            for row in range(2):
+                t = 2 * half + row
+                nc.vector.tensor_scalar(out=dz2_rows[g][:, t * H:(t + 1) * H], in0=masked[g, half][:, row * H:(row + 1) * H],
+                                        scalar1=dinv[:, g * PACK + t:g * PACK + t + 1], scalar2=None, op0=ALU.mult)
+
+        def pack_dz2(g):
+            interleave(dz2[g][:], dz2_rows[g][:].rearrange("p (t c i) -> p c t i", t=PACK, i=4))
+
+        def quantise_dz2(g):
+            quantise(dz2[g][:], dz2_codes[g], dz2_scales[g], E5M2, 0, H)
+
+        def dh_pass(g, c, s, first):
+            if first:
+                dh[c, s] = bank(PACK * c + s, "dh%d%d" % (c, s))
+            cols = slice(s * P, (s + 1) * P)
+            nc.tensor.matmul_mx(out=dh[c, s][:], lhsT=adj_codes[g, c][:, cols].bitcast(E4M3), lhsT_scale=adj_scales[g, c][:, cols],
+                                rhs=dz2_codes[g][:].bitcast(E5M2), rhs_scale=dz2_scales[g][:], start=first, stop=not first)
+
+        def round_dz1(engine, c, s):
+            src = dh[c, s][:].rearrange("p (w u e) -> p u w e", u=2, e=2)
+            dst = dz1_rows[c][:, s * H:(s + 1) * H].rearrange("p (u w e) -> p u w e", u=2, e=2)
+            factor = dinv[:, c * PACK + s:c * PACK + s + 1]
+            if engine == "scalar":
+                nc.scalar.activation(out=dst, in_=src, func=ACT.Copy, scale=factor)
+            else:
+                nc.vector.tensor_scalar(out=dst, in0=src, scalar1=factor, scalar2=None, op0=ALU.mult)
+
+        def flip_dz1(c, s):
+            half, row = divmod(s, 2)
+            if (c, half) not in flipped:
+                flipped[c, half] = bank(PACK * c + 2 * half, "flipped%d%d" % (c, half))
+            words = dz1_rows[c][:, s * H:(s + 1) * H].bitcast(F32)
+            for u in range(2):
+                at = (2 * row + u) * P
+                nc.tensor.transpose(flipped[c, half][:, at:at + P], words[:, u * P:(u + 1) * P], ident[:])
+
+        def copy(engine, dst, src):
+            if engine == "scalar":
+                nc.scalar.copy(out=dst, in_=src)
+            else:
+                nc.vector.tensor_copy(out=dst, in_=src)
+
+        def pack_feat(engine, c, half):
+            copy(engine, dz1_by_feat[c, half][:].bitcast(F32).rearrange("p (s m u) -> p s m u", s=2, u=2),
+                 flipped[c, half][:].rearrange("p (s u m) -> p s m u", s=2, u=2))
+
+        def quantise_feat(c, half):
+            quantise(dz1_by_feat[c, half][:], feat_codes[c, half], feat_scales[c, half], E5M2, 0, 2 * P)
+
+        def dx_pass(c, s):
+            half, row = divmod(s, 2)
+            if s == 0:
+                dx_ps[c] = bank(PACK * c + 1, "dx%d" % c)
+            cols = slice(row * P, (row + 1) * P)
+            window = slice((PACK - 1 - s) * D, (2 * PACK - 1 - s) * D)
+            nc.tensor.matmul_mx(out=dx_ps[c][:], lhsT=feat_codes[c, half][:, cols].bitcast(E5M2), lhsT_scale=feat_scales[c, half][:, cols],
+                                rhs=w_codes[:, window].bitcast(E4M3), rhs_scale=w_scales[:, window],
+                                start=(s == 0), stop=(s == PACK - 1))
+
+        def store_dx(engine, c):
+            copy(engine, dx_sb[c][:], dx_ps[c][:])
+            nc.sync.dma_start(out=out_0[c * PASS:(c + 1) * PASS, :].rearrange("(m s) d -> m (s d)", s=PACK), in_=dx_sb[c][:])
+
+        def pack_node(c, half):
+            src = dz1_rows[c][:].rearrange("p (s k c i) -> p k c s i", s=PACK, k=2, i=4)[:, half]
+            interleave(dz1_by_node[c][:, half * 2 * H:(half + 1) * 2 * H], src)
+
+        def quantise_node(c, half):
+            quantise(dz1_by_node[c][:, half * 2 * H:(half + 1) * 2 * H], node_codes[c], node_scales[c], E5M2, half * 2 * P, 2 * P)
+
+        def dw_pass(c):
+            if c == 0:
+                dw_ps[0] = bank(PACK - 1, "dw")
+            cols = slice(c * D, (c + 1) * D)
+            nc.tensor.matmul_mx(out=dw_ps[0][:], lhsT=x_codes[:, cols].bitcast(E4M3), lhsT_scale=x_scales[:, cols],
+                                rhs=node_codes[c][:].bitcast(E5M2), rhs_scale=node_scales[c][:],
+                                start=(c == 0), stop=(c == PASSES - 1))
+
+        def store_dw(engine):
+            copy(engine, dw_sb[:].rearrange("p (w u e) -> p w u e", u=2, e=2),
+                 dw_ps[0][:].rearrange("p (u w e) -> p w u e", u=2, e=2))
+            nc.sync.dma_start(out=out_1, in_=dw_sb[:])
+
+        def pack_x():
+            nc.vector.tensor_copy(out=x_packed[:].rearrange("p (c k i s) -> p c k s i", c=PASSES, i=4, s=PACK),
+                                  in_=x_rows[:].rearrange("p (c s k i) -> p c k s i", c=PASSES, s=PACK, i=4))
+
+        def quantise_x():
+            quantise(x_packed[:], x_codes, x_scales, E4M3, 0, PASSES * D)
+
+        def flip_w():
+            flipped["w"] = bank(2 * PACK - 1, "flipped_w")
+            words = w_rows[:].bitcast(F32)
+            for u in range(2):
+                nc.tensor.transpose(flipped["w"][:, u * P:(u + 1) * P], words[:, u:2 * P:2], ident[:])
+
+        def pack_w(engine):
+            copy(engine, w_packed[:].bitcast(F32).rearrange("p (d u) -> p d u", u=2),
+                 flipped["w"][:, 0:2 * P].rearrange("p (u d) -> p d u", u=2))
+
+        def quantise_w():
+            quantise(w_packed[:], w_codes, w_scales, E4M3, (PACK - 1) * D, D)
+
+        S, V = "scalar", "vector"
+        load_dist(0, 0, 0)
+        constants()
+        load_x()
+        load_dist(0, 0, 1)
+        load_z(0, 0)
+        load_grad(0, 0)
+        load_dist(0, 1, 0)
+        load_z(0, 1)
+        load_grad(0, 1)
+        load_dist(0, 1, 1)
+        load_w()
+        load_z(1, 0)
+        load_grad(1, 0)
+        load_dist(1, 0, 0)
+        load_z(1, 1)
+        load_grad(1, 1)
+        load_dist(1, 0, 1)
+        load_dist(1, 1, 0)
+        load_dist(1, 1, 1)
+        inverse_root(0, 0, 0)
+        inverse_root(0, 0, 1)
+        pack_x()
+        self_loops(0, 0)
+        quantise_x()
+        self_loops(0, 1)
+        mask_grad(0, 0)
+        square(S, 0, 0, 0)
+        inverse_root(0, 1, 0)
+        square(S, 0, 0, 1)
+        square(S, 0, 0, 2)
+        square(S, 0, 0, 3)
+        inverse_root(0, 1, 1)
+        scale_grad(0, 0)
+        mask_grad(0, 1)
+        flip_w()
+        pack_w(V)
+        scale_grad(0, 1)
+        quantise_adj(0, 0, 0, 4)
+        pack_dz2(0)
+        mask_grad(1, 0)
+        quantise_dz2(0)
+        scale_grad(1, 0)
+        square(S, 0, 1, 0)
+        square(S, 0, 1, 1)
+        square(S, 0, 1, 2)
+        square(S, 0, 1, 3)
+        inverse_root(1, 0, 0)
+        inverse_root(1, 0, 1)
+        dh_pass(0, 0, 0, True)
+        dh_pass(0, 0, 1, True)
+        dh_pass(0, 0, 2, True)
+        dh_pass(0, 0, 3, True)
+        mask_grad(1, 1)
+        quantise_adj(0, 1, 0, 4)
+        scale_grad(1, 1)
+        quantise_w()
+        pack_dz2(1)
+        dh_pass(0, 1, 0, True)
+        dh_pass(0, 1, 1, True)
+        dh_pass(0, 1, 2, True)
+        dh_pass(0, 1, 3, True)
+        square(S, 1, 0, 0)
+        square(S, 1, 0, 1)
+        square(S, 1, 0, 2)
+        square(S, 1, 0, 3)
+        quantise_adj(1, 0, 0, 2)
+        quantise_dz2(1)
+        quantise_adj(1, 0, 2, 4)
+        inverse_root(1, 1, 0)
+        inverse_root(1, 1, 1)
+        dh_pass(1, 0, 0, False)
+        dh_pass(1, 0, 1, False)
+        dh_pass(1, 0, 2, False)
+        dh_pass(1, 0, 3, False)
+        self_loops(1, 0)
+        round_dz1(V, 0, 0)
+        self_loops(1, 1)
+        round_dz1(V, 0, 1)
+        round_dz1(S, 0, 2)
+        square(S, 1, 1, 0)
+        square(S, 1, 1, 1)
+        round_dz1(V, 0, 3)
+        square(V, 1, 1, 2)
+        square(S, 1, 1, 3)
+        flip_dz1(0, 0)
+        flip_dz1(0, 1)
+        flip_dz1(0, 2)
+        flip_dz1(0, 3)
+        quantise_adj(1, 1, 0, 2)
+        pack_node(0, 0)
+        quantise_adj(1, 1, 2, 4)
+        pack_node(0, 1)
+        dh_pass(1, 1, 0, False)
+        dh_pass(1, 1, 1, False)
+        dh_pass(1, 1, 2, False)
+        dh_pass(1, 1, 3, False)
+        pack_feat(S, 0, 0)
+        pack_feat(S, 0, 1)
+        round_dz1(S, 1, 0)
+        round_dz1(S, 1, 1)
+        quantise_feat(0, 0)
+        round_dz1(V, 1, 3)
+        round_dz1(S, 1, 2)
+        quantise_feat(0, 1)
+        quantise_node(0, 0)
+        flip_dz1(1, 0)
+        flip_dz1(1, 1)
+        dx_pass(0, 0)
+        flip_dz1(1, 3)
+        flip_dz1(1, 2)
+        dx_pass(0, 1)
+        dx_pass(0, 2)
+        dx_pass(0, 3)
+        pack_node(1, 0)
+        pack_feat(S, 1, 0)
+        quantise_node(0, 1)
+        pack_node(1, 1)
+        pack_feat(S, 1, 1)
+        quantise_feat(1, 0)
+        quantise_node(1, 0)
+        quantise_feat(1, 1)
+        quantise_node(1, 1)
+        store_dx(S, 0)
+        dw_pass(0)
+        dx_pass(1, 0)
+        dx_pass(1, 1)
+        dx_pass(1, 2)
+        dx_pass(1, 3)
+        dw_pass(1)
+        store_dx(S, 1)
+        store_dw(V)

@@ -21,7 +21,7 @@ P = 128
 PACK = 4
 PASS = P * PACK
 PASSES = N // PASS
-HUGE = 2.0 ** 120
+CAP = 2.0 ** 22
 
 
 def tile_ensemblenet_pa_v_kernel(tc, d1_t, d1_f, xt, xf, W_gt, W_gf, b_g, z, dinv_t, grad_out, out_0, out_1):
@@ -45,9 +45,8 @@ def tile_ensemblenet_pa_v_kernel(tc, d1_t, d1_f, xt, xf, W_gt, W_gf, b_g, z, din
         adj_scales = {(g, c): sbuf("adj_scales%d%d" % (g, c), PASS, U8) for g, c in pairs}
         halves = [(g, half) for g in range(PASSES) for half in range(2)]
         z_sb = {k: sbuf("z%d%d" % k, 2 * H, F32) for k in halves}
-        grad = {k: sbuf("grad%d%d" % k, 2 * H, BF16) for k in halves}
-        masked = {k: sbuf("masked%d%d" % k, 2 * H, BF16) for k in halves}
-        dz2_rows = [sbuf("dz2_rows%d" % g, PACK * H, BF16) for g in range(PASSES)]
+        grad = [sbuf("grad%d" % g, PACK * H, BF16) for g in range(PASSES)]
+        gate = [sbuf("gate%d" % g, PACK * H, F32) for g in range(PASSES)]
         dz2 = [sbuf("dz2_%d" % g, PACK * H, BF16) for g in range(PASSES)]
         dz2_codes = [sbuf("dz2_codes%d" % g, H, U32) for g in range(PASSES)]
         dz2_scales = [sbuf("dz2_scales%d" % g, H, U8) for g in range(PASSES)]
@@ -70,6 +69,7 @@ def tile_ensemblenet_pa_v_kernel(tc, d1_t, d1_f, xt, xf, W_gt, W_gf, b_g, z, din
         ident = sbuf("ident", P, F32)
         loop_cap = sbuf("loop_cap", PASS, F32)
         warm = sbuf("warm", 8, F32)
+        cap_row = sbuf("cap_row", PACK, F32)
         dx_sb = [sbuf("dx_sb%d" % c, PACK * D, F32) for c in range(PASSES)]
         dw_sb = sbuf("dw_sb", H, F32)
         dh, flipped, dx_ps, dw_ps = {}, {}, {}, {}
@@ -84,8 +84,12 @@ def tile_ensemblenet_pa_v_kernel(tc, d1_t, d1_f, xt, xf, W_gt, W_gf, b_g, z, din
         def load_z(g, half):
             nc.sync.dma_start(out=z_sb[g, half][:].rearrange("p (t h) -> p t h", t=2), in_=rows_of(z, g, half))
 
-        def load_grad(g, half):
-            nc.sync.dma_start(out=grad[g, half][:].rearrange("p (t h) -> p t h", t=2), in_=rows_of(grad_out, g, half))
+        def load_grad(g):
+            nc.sync.dma_start(out=grad[g][:], in_=grad_out[g * PASS:(g + 1) * PASS, :].rearrange("(p t) h -> p (t h)", t=PACK))
+
+        def load_dinv():
+            nc.sync.dma_start(out=dinv[:].rearrange("p (g t) -> p g t", g=PASSES),
+                              in_=dinv_t.rearrange("(g p t) -> p g t", g=PASSES, t=PACK))
 
         def load_x():
             nc.sync.dma_start(out=x_rows[:].rearrange("p (c w) -> p c w", c=PASSES),
@@ -95,16 +99,17 @@ def tile_ensemblenet_pa_v_kernel(tc, d1_t, d1_f, xt, xf, W_gt, W_gf, b_g, z, din
             nc.sync.dma_start(out=w_rows[:], in_=W_gt)
 
         def constants():
-            nc.scalar.dma_start(out=dinv[:].rearrange("p (g t) -> p g t", g=PASSES),
-                                in_=dinv_t.rearrange("(g p t) -> p g t", g=PASSES, t=PACK))
+            make_identity(nc, ident[:])
             nc.vector.memset(warm[:], 1.0)
             nc.scalar.activation(out=warm[:, 0:1], in_=warm[:, 0:1], func=ACT.Abs_reciprocal_sqrt)
-            nc.vector.memset(loop_cap[:], HUGE)
-            nc.gpsimd.affine_select(out=loop_cap[:], in_=loop_cap[:], pattern=[[PACK, P], [1, 2], [-1, 2]],
-                                    compare_op=ALU.not_equal, fill=-1.0, base=0, channel_multiplier=-PACK)
-            make_identity(nc, ident[:])
+            nc.vector.memset(cap_row[:], CAP)
+            nc.vector.memset(cap_row[:, 1:3], 2 * CAP + 1)
             nc.vector.memset(w_codes[:], 0)
             nc.vector.memset(w_scales[:].bitcast(U32), 0)
+            nc.vector.scalar_tensor_tensor(out=loop_cap[:].rearrange("p (m q) -> p m q", q=PACK),
+                                           in0=ident[:].unsqueeze(2).to_broadcast([P, P, PACK]), scalar=-(CAP + 1),
+                                           in1=cap_row[:].unsqueeze(1).to_broadcast([P, P, PACK]),
+                                           op0=ALU.mult, op1=ALU.add)
 
         def inverse_root(g, c, half):
             nc.scalar.activation(out=root[g, c][:, half * 2 * PASS:(half + 1) * 2 * PASS].rearrange("p (j t) -> p j t", t=2),
@@ -133,18 +138,18 @@ def tile_ensemblenet_pa_v_kernel(tc, d1_t, d1_f, xt, xf, W_gt, W_gf, b_g, z, din
         def interleave(dst, src):
             nc.vector.tensor_copy(out=dst.rearrange("p (c i t) -> p c t i", i=4, t=PACK), in_=src)
 
-        def mask_grad(g, half):
-            nc.vector.scalar_tensor_tensor(out=masked[g, half][:], in0=z_sb[g, half][:], scalar=0.0, in1=grad[g, half][:],
-                                           op0=ALU.is_gt, op1=ALU.mult)
-
-        def scale_grad(g, half):
+        def gate_rows(g, half):
             for row in range(2):
                 t = 2 * half + row
-                nc.vector.tensor_scalar(out=dz2_rows[g][:, t * H:(t + 1) * H], in0=masked[g, half][:, row * H:(row + 1) * H],
-                                        scalar1=dinv[:, g * PACK + t:g * PACK + t + 1], scalar2=None, op0=ALU.mult)
+                nc.vector.tensor_scalar(out=gate[g][:, t * H:(t + 1) * H], in0=z_sb[g, half][:, row * H:(row + 1) * H],
+                                        scalar1=0.0, scalar2=dinv[:, g * PACK + t:g * PACK + t + 1],
+                                        op0=ALU.is_gt, op1=ALU.mult)
 
-        def pack_dz2(g):
-            interleave(dz2[g][:], dz2_rows[g][:].rearrange("p (t c i) -> p c t i", t=PACK, i=4))
+        def round_dz2(g, half):
+            order = "p (t k c i) -> p k c t i"
+            nc.vector.tensor_tensor(out=dz2[g][:, half * 2 * H:(half + 1) * 2 * H].rearrange("p (c i t) -> p c t i", i=2, t=PACK),
+                                    in0=gate[g][:].rearrange(order, t=PACK, k=2, i=2)[:, half],
+                                    in1=grad[g][:].rearrange(order, t=PACK, k=2, i=2)[:, half], op=ALU.mult)
 
         def quantise_dz2(g):
             quantise(dz2[g][:], dz2_codes[g], dz2_scales[g], E5M2, 0, H)
@@ -244,61 +249,62 @@ def tile_ensemblenet_pa_v_kernel(tc, d1_t, d1_f, xt, xf, W_gt, W_gf, b_g, z, din
         S, V = "scalar", "vector"
         load_dist(0, 0, 0)
         constants()
-        load_x()
         load_dist(0, 0, 1)
+        load_dinv()
         load_z(0, 0)
-        load_grad(0, 0)
-        load_dist(0, 1, 0)
+        load_dist(1, 1, 0)
         load_z(0, 1)
-        load_grad(0, 1)
+        load_grad(0)
+        load_dist(1, 1, 1)
+        load_dist(0, 1, 0)
+        load_z(1, 0)
         load_dist(0, 1, 1)
         load_w()
-        load_z(1, 0)
-        load_grad(1, 0)
-        load_dist(1, 0, 0)
         load_z(1, 1)
-        load_grad(1, 1)
+        load_grad(1)
+        load_dist(1, 0, 0)
         load_dist(1, 0, 1)
-        load_dist(1, 1, 0)
-        load_dist(1, 1, 1)
+        load_x()
         inverse_root(0, 0, 0)
         inverse_root(0, 0, 1)
-        pack_x()
         self_loops(0, 0)
-        quantise_x()
         self_loops(0, 1)
-        mask_grad(0, 0)
+        gate_rows(0, 0)
         square(S, 0, 0, 0)
-        inverse_root(0, 1, 0)
-        square(S, 0, 0, 1)
+        inverse_root(1, 1, 0)
+        square(V, 0, 0, 1)
         square(S, 0, 0, 2)
         square(S, 0, 0, 3)
+        inverse_root(1, 1, 1)
+        inverse_root(0, 1, 0)
         inverse_root(0, 1, 1)
-        scale_grad(0, 0)
-        mask_grad(0, 1)
-        flip_w()
-        pack_w(V)
-        scale_grad(0, 1)
+        gate_rows(0, 1)
+        self_loops(1, 0)
+        round_dz2(0, 0)
+        round_dz2(0, 1)
         quantise_adj(0, 0, 0, 4)
-        pack_dz2(0)
-        mask_grad(1, 0)
+        self_loops(1, 1)
         quantise_dz2(0)
-        scale_grad(1, 0)
+        gate_rows(1, 0)
+        flip_w()
         square(S, 0, 1, 0)
         square(S, 0, 1, 1)
         square(S, 0, 1, 2)
         square(S, 0, 1, 3)
+        square(V, 1, 1, 0)
+        gate_rows(1, 1)
+        pack_w(V)
+        round_dz2(1, 0)
+        round_dz2(1, 1)
+        quantise_adj(0, 1, 0, 4)
+        quantise_dz2(1)
+        quantise_w()
         inverse_root(1, 0, 0)
         inverse_root(1, 0, 1)
         dh_pass(0, 0, 0, True)
         dh_pass(0, 0, 1, True)
         dh_pass(0, 0, 2, True)
         dh_pass(0, 0, 3, True)
-        mask_grad(1, 1)
-        quantise_adj(0, 1, 0, 4)
-        scale_grad(1, 1)
-        quantise_w()
-        pack_dz2(1)
         dh_pass(0, 1, 0, True)
         dh_pass(0, 1, 1, True)
         dh_pass(0, 1, 2, True)
@@ -307,67 +313,63 @@ def tile_ensemblenet_pa_v_kernel(tc, d1_t, d1_f, xt, xf, W_gt, W_gf, b_g, z, din
         square(S, 1, 0, 1)
         square(S, 1, 0, 2)
         square(S, 1, 0, 3)
+        pack_x()
+        square(V, 1, 1, 1)
         quantise_adj(1, 0, 0, 2)
-        quantise_dz2(1)
+        quantise_x()
         quantise_adj(1, 0, 2, 4)
-        inverse_root(1, 1, 0)
-        inverse_root(1, 1, 1)
+        quantise_adj(1, 1, 0, 2)
+        square(S, 1, 1, 2)
+        square(S, 1, 1, 3)
         dh_pass(1, 0, 0, False)
         dh_pass(1, 0, 1, False)
         dh_pass(1, 0, 2, False)
         dh_pass(1, 0, 3, False)
-        self_loops(1, 0)
+        dh_pass(1, 1, 0, False)
+        dh_pass(1, 1, 1, False)
         round_dz1(V, 0, 0)
-        self_loops(1, 1)
-        round_dz1(V, 0, 1)
-        round_dz1(S, 0, 2)
-        square(S, 1, 1, 0)
-        square(S, 1, 1, 1)
+        quantise_adj(1, 1, 2, 4)
+        round_dz1(S, 0, 1)
         round_dz1(V, 0, 3)
-        square(V, 1, 1, 2)
-        square(S, 1, 1, 3)
+        round_dz1(S, 0, 2)
+        dh_pass(1, 1, 2, False)
+        dh_pass(1, 1, 3, False)
         flip_dz1(0, 0)
         flip_dz1(0, 1)
         flip_dz1(0, 2)
         flip_dz1(0, 3)
-        quantise_adj(1, 1, 0, 2)
-        pack_node(0, 0)
-        quantise_adj(1, 1, 2, 4)
-        pack_node(0, 1)
-        dh_pass(1, 1, 0, False)
-        dh_pass(1, 1, 1, False)
-        dh_pass(1, 1, 2, False)
-        dh_pass(1, 1, 3, False)
-        pack_feat(S, 0, 0)
-        pack_feat(S, 0, 1)
         round_dz1(S, 1, 0)
-        round_dz1(S, 1, 1)
-        quantise_feat(0, 0)
-        round_dz1(V, 1, 3)
+        round_dz1(V, 1, 1)
+        pack_feat(S, 0, 0)
+        pack_node(0, 0)
         round_dz1(S, 1, 2)
-        quantise_feat(0, 1)
+        pack_node(0, 1)
+        round_dz1(S, 1, 3)
+        quantise_feat(0, 0)
+        pack_feat(S, 0, 1)
         quantise_node(0, 0)
         flip_dz1(1, 0)
         flip_dz1(1, 1)
         dx_pass(0, 0)
-        flip_dz1(1, 3)
-        flip_dz1(1, 2)
         dx_pass(0, 1)
-        dx_pass(0, 2)
-        dx_pass(0, 3)
-        pack_node(1, 0)
+        flip_dz1(1, 2)
+        flip_dz1(1, 3)
         pack_feat(S, 1, 0)
         quantise_node(0, 1)
+        pack_node(1, 0)
+        quantise_feat(0, 1)
         pack_node(1, 1)
         pack_feat(S, 1, 1)
         quantise_feat(1, 0)
-        quantise_node(1, 0)
-        quantise_feat(1, 1)
-        quantise_node(1, 1)
-        store_dx(S, 0)
+        dx_pass(0, 2)
+        dx_pass(0, 3)
         dw_pass(0)
         dx_pass(1, 0)
         dx_pass(1, 1)
+        quantise_feat(1, 1)
+        quantise_node(1, 0)
+        quantise_node(1, 1)
+        store_dx(S, 0)
         dx_pass(1, 2)
         dx_pass(1, 3)
         dw_pass(1)

@@ -63,14 +63,14 @@ def tile_ensemblenet_pa_v_kernel(tc, d1_t, d1_f, xt, xf, W_gt, W_gf, b_g, z, din
         x_scales = sbuf("x_scales", PASSES * D, U8)
         w_rows = sbuf("w_rows", H, BF16)
         w_packed = sbuf("w_packed", PACK * D, BF16)
-        w_codes = sbuf("w_codes", (2 * PACK - 1) * D, U32)
-        w_scales = sbuf("w_scales", (2 * PACK - 1) * D, U8)
+        w_codes = sbuf("w_codes", (PACK + 1) * D, U32)
+        w_scales = sbuf("w_scales", (PACK + 1) * D, U8)
         dinv = sbuf("dinv", PASSES * PACK, F32)
         ident = sbuf("ident", P, F32)
         loop_cap = sbuf("loop_cap", PASS, F32)
         warm = sbuf("warm", 8, F32)
         cap_row = sbuf("cap_row", PACK, F32)
-        dx_sb = [sbuf("dx_sb%d" % c, PACK * D, F32) for c in range(PASSES)]
+        dx_sb = {k: sbuf("dx_sb%d%d" % k, 2 * D, F32) for k in halves}
         dw_sb = sbuf("dw_sb", H, F32)
         dh, flipped, dx_ps, dw_ps = {}, {}, {}, {}
 
@@ -194,17 +194,17 @@ def tile_ensemblenet_pa_v_kernel(tc, d1_t, d1_f, xt, xf, W_gt, W_gf, b_g, z, din
 
         def dx_pass(c, s):
             half, row = divmod(s, 2)
-            if s == 0:
-                dx_ps[c] = bank(PACK * c + 1, "dx%d" % c)
+            if row == 0:
+                dx_ps[c, half] = bank(PACK * c + 2 * half + 1, "dx%d%d" % (c, half))
             cols = slice(row * P, (row + 1) * P)
-            window = slice((PACK - 1 - s) * D, (2 * PACK - 1 - s) * D)
-            nc.tensor.matmul_mx(out=dx_ps[c][:], lhsT=feat_codes[c, half][:, cols].bitcast(E5M2), lhsT_scale=feat_scales[c, half][:, cols],
+            window = slice((1 - row) * D, (1 - row + PACK) * D)
+            nc.tensor.matmul_mx(out=dx_ps[c, half][:], lhsT=feat_codes[c, half][:, cols].bitcast(E5M2), lhsT_scale=feat_scales[c, half][:, cols],
                                 rhs=w_codes[:, window].bitcast(E4M3), rhs_scale=w_scales[:, window],
-                                start=(s == 0), stop=(s == PACK - 1))
+                                start=(row == 0), stop=(row == 1))
 
-        def store_dx(engine, c):
-            copy(engine, dx_sb[c][:], dx_ps[c][:])
-            nc.sync.dma_start(out=out_0[c * PASS:(c + 1) * PASS, :].rearrange("(m s) d -> m (s d)", s=PACK), in_=dx_sb[c][:])
+        def store_dx(engine, c, half):
+            copy(engine, dx_sb[c, half][:], dx_ps[c, half][:, 0:2 * D])
+            nc.sync.dma_start(out=rows_of(out_0, c, half), in_=dx_sb[c, half][:].rearrange("p (s d) -> p s d", s=2))
 
         def pack_node(c, half):
             src = dz1_rows[c][:].rearrange("p (s k c i) -> p k c s i", s=PACK, k=2, i=4)[:, half]
@@ -213,13 +213,13 @@ def tile_ensemblenet_pa_v_kernel(tc, d1_t, d1_f, xt, xf, W_gt, W_gf, b_g, z, din
         def quantise_node(c, half):
             quantise(dz1_by_node[c][:, half * 2 * H:(half + 1) * 2 * H], node_codes[c], node_scales[c], E5M2, half * 2 * P, 2 * P)
 
-        def dw_pass(c):
-            if c == 0:
-                dw_ps[0] = bank(PACK - 1, "dw")
+        def dw_pass(c, first):
+            if first:
+                dw_ps[0] = bank(PACK * c, "dw")
             cols = slice(c * D, (c + 1) * D)
             nc.tensor.matmul_mx(out=dw_ps[0][:], lhsT=x_codes[:, cols].bitcast(E4M3), lhsT_scale=x_scales[:, cols],
                                 rhs=node_codes[c][:].bitcast(E5M2), rhs_scale=node_scales[c][:],
-                                start=(c == 0), stop=(c == PASSES - 1))
+                                start=first, stop=not first)
 
         def store_dw(engine):
             copy(engine, dw_sb[:].rearrange("p (w u e) -> p w u e", u=2, e=2),
@@ -234,7 +234,7 @@ def tile_ensemblenet_pa_v_kernel(tc, d1_t, d1_f, xt, xf, W_gt, W_gf, b_g, z, din
             quantise(x_packed[:], x_codes, x_scales, E4M3, 0, PASSES * D)
 
         def flip_w():
-            flipped["w"] = bank(2 * PACK - 1, "flipped_w")
+            flipped["w"] = bank(2 * PACK - 2, "flipped_w")
             words = w_rows[:].bitcast(F32)
             for u in range(2):
                 nc.tensor.transpose(flipped["w"][:, u * P:(u + 1) * P], words[:, u:2 * P:2], ident[:])
@@ -244,134 +244,135 @@ def tile_ensemblenet_pa_v_kernel(tc, d1_t, d1_f, xt, xf, W_gt, W_gf, b_g, z, din
                  flipped["w"][:, 0:2 * P].rearrange("p (u d) -> p d u", u=2))
 
         def quantise_w():
-            quantise(w_packed[:], w_codes, w_scales, E4M3, (PACK - 1) * D, D)
+            quantise(w_packed[:], w_codes, w_scales, E4M3, D, D)
 
         S, V = "scalar", "vector"
         load_dist(0, 0, 0)
         constants()
         load_dist(0, 0, 1)
         load_dinv()
-        load_z(0, 0)
         load_dist(1, 1, 0)
+        load_z(0, 0)
         load_z(0, 1)
+        load_dist(0, 1, 0)
+        load_dist(0, 1, 1)
         load_grad(0)
         load_dist(1, 1, 1)
-        load_dist(0, 1, 0)
         load_z(1, 0)
-        load_dist(0, 1, 1)
-        load_w()
         load_z(1, 1)
+        load_w()
         load_grad(1)
         load_dist(1, 0, 0)
         load_dist(1, 0, 1)
         load_x()
         inverse_root(0, 0, 0)
         inverse_root(0, 0, 1)
+        inverse_root(1, 1, 0)
         self_loops(0, 0)
         self_loops(0, 1)
         gate_rows(0, 0)
         square(S, 0, 0, 0)
-        inverse_root(1, 1, 0)
-        square(V, 0, 0, 1)
-        square(S, 0, 0, 2)
-        square(S, 0, 0, 3)
-        inverse_root(1, 1, 1)
+        square(S, 0, 0, 1)
+        square(V, 0, 0, 2)
+        gate_rows(0, 1)
+        square(V, 0, 0, 3)
+        self_loops(1, 0)
+        quantise_adj(0, 0, 0, 4)
         inverse_root(0, 1, 0)
         inverse_root(0, 1, 1)
-        gate_rows(0, 1)
-        self_loops(1, 0)
-        round_dz2(0, 0)
-        round_dz2(0, 1)
-        quantise_adj(0, 0, 0, 4)
-        self_loops(1, 1)
-        quantise_dz2(0)
-        gate_rows(1, 0)
-        flip_w()
+        inverse_root(1, 1, 1)
         square(S, 0, 1, 0)
         square(S, 0, 1, 1)
         square(S, 0, 1, 2)
         square(S, 0, 1, 3)
-        square(V, 1, 1, 0)
+        round_dz2(0, 0)
+        round_dz2(0, 1)
+        self_loops(1, 1)
+        quantise_dz2(0)
+        gate_rows(1, 0)
         gate_rows(1, 1)
-        pack_w(V)
-        round_dz2(1, 0)
-        round_dz2(1, 1)
         quantise_adj(0, 1, 0, 4)
-        quantise_dz2(1)
-        quantise_w()
-        inverse_root(1, 0, 0)
-        inverse_root(1, 0, 1)
+        square(S, 1, 1, 0)
+        square(S, 1, 1, 1)
+        square(S, 1, 1, 2)
+        square(S, 1, 1, 3)
+        flip_w()
         dh_pass(0, 0, 0, True)
         dh_pass(0, 0, 1, True)
         dh_pass(0, 0, 2, True)
         dh_pass(0, 0, 3, True)
+        round_dz2(1, 0)
+        round_dz2(1, 1)
+        pack_w(V)
+        quantise_dz2(1)
+        quantise_adj(1, 1, 0, 4)
         dh_pass(0, 1, 0, True)
         dh_pass(0, 1, 1, True)
         dh_pass(0, 1, 2, True)
         dh_pass(0, 1, 3, True)
-        square(S, 1, 0, 0)
-        square(S, 1, 0, 1)
-        square(S, 1, 0, 2)
-        square(S, 1, 0, 3)
-        pack_x()
-        square(V, 1, 1, 1)
-        quantise_adj(1, 0, 0, 2)
-        quantise_x()
-        quantise_adj(1, 0, 2, 4)
-        quantise_adj(1, 1, 0, 2)
-        square(S, 1, 1, 2)
-        square(S, 1, 1, 3)
-        dh_pass(1, 0, 0, False)
-        dh_pass(1, 0, 1, False)
-        dh_pass(1, 0, 2, False)
-        dh_pass(1, 0, 3, False)
+        inverse_root(1, 0, 0)
+        inverse_root(1, 0, 1)
         dh_pass(1, 1, 0, False)
         dh_pass(1, 1, 1, False)
-        round_dz1(V, 0, 0)
-        quantise_adj(1, 1, 2, 4)
-        round_dz1(S, 0, 1)
-        round_dz1(V, 0, 3)
-        round_dz1(S, 0, 2)
         dh_pass(1, 1, 2, False)
         dh_pass(1, 1, 3, False)
-        flip_dz1(0, 0)
-        flip_dz1(0, 1)
-        flip_dz1(0, 2)
-        flip_dz1(0, 3)
-        round_dz1(S, 1, 0)
-        round_dz1(V, 1, 1)
-        pack_feat(S, 0, 0)
-        pack_node(0, 0)
+        square(S, 1, 0, 0)
+        square(S, 1, 0, 1)
+        pack_x()
+        square(V, 1, 0, 2)
+        quantise_w()
+        square(S, 1, 0, 3)
+        quantise_x()
+        quantise_adj(1, 0, 0, 2)
+        round_dz1(V, 1, 0)
+        quantise_adj(1, 0, 2, 4)
+        round_dz1(S, 1, 1)
         round_dz1(S, 1, 2)
-        pack_node(0, 1)
-        round_dz1(S, 1, 3)
-        quantise_feat(0, 0)
-        pack_feat(S, 0, 1)
-        quantise_node(0, 0)
+        round_dz1(V, 1, 3)
+        dh_pass(1, 0, 0, False)
+        dh_pass(1, 0, 1, False)
         flip_dz1(1, 0)
         flip_dz1(1, 1)
-        dx_pass(0, 0)
-        dx_pass(0, 1)
+        dh_pass(1, 0, 2, False)
+        dh_pass(1, 0, 3, False)
         flip_dz1(1, 2)
         flip_dz1(1, 3)
+        round_dz1(S, 0, 0)
+        round_dz1(S, 0, 1)
         pack_feat(S, 1, 0)
-        quantise_node(0, 1)
+        round_dz1(S, 0, 2)
+        round_dz1(S, 0, 3)
         pack_node(1, 0)
-        quantise_feat(0, 1)
         pack_node(1, 1)
-        pack_feat(S, 1, 1)
         quantise_feat(1, 0)
-        dx_pass(0, 2)
-        dx_pass(0, 3)
-        dw_pass(0)
-        dx_pass(1, 0)
-        dx_pass(1, 1)
-        quantise_feat(1, 1)
         quantise_node(1, 0)
         quantise_node(1, 1)
-        store_dx(S, 0)
+        flip_dz1(0, 0)
+        flip_dz1(0, 1)
+        dx_pass(1, 0)
+        dx_pass(1, 1)
+        flip_dz1(0, 2)
+        flip_dz1(0, 3)
+        dw_pass(1, True)
+        pack_feat(S, 0, 0)
+        pack_feat(S, 1, 1)
+        pack_feat(S, 0, 1)
+        pack_node(0, 0)
+        quantise_feat(0, 0)
+        pack_node(0, 1)
+        quantise_feat(1, 1)
+        quantise_node(0, 0)
+        quantise_node(0, 1)
+        quantise_feat(0, 1)
+        dx_pass(0, 0)
+        dx_pass(0, 1)
         dx_pass(1, 2)
         dx_pass(1, 3)
-        dw_pass(1)
-        store_dx(S, 1)
+        dw_pass(0, False)
+        dx_pass(0, 2)
+        dx_pass(0, 3)
+        store_dx(S, 1, 0)
+        store_dx(S, 0, 0)
+        store_dx(S, 1, 1)
         store_dw(V)
+        store_dx(S, 0, 1)

@@ -6,7 +6,7 @@ from concourse.masks import make_identity
 N, D, H = 1024, 128, 512
 EPS = 1e-5
 FLOPS = 2 * N * N * H + 2 * N * H * D + 2 * N * D * H
-BYTES = 2 * N * N + 2 * N * D + 2 * D * H + 4 * N * H + 4 * N + 2 * N * H + 4 * N * D + 4 * D * H
+BYTES = 2 * (N * N + N * D + D * H + N * H) + 4 * (N * H + N + N * D + D * H)
 
 F32 = mybir.dt.float32
 BF16 = mybir.dt.bfloat16
@@ -18,10 +18,11 @@ ACT = mybir.ActivationFunctionType
 ALU = mybir.AluOpType
 
 P = 128
-PACK = 4
-PASS = P * PACK
+SLOTS = 4
+PASS = P * SLOTS
 PASSES = N // PASS
 CAP = 2.0 ** 22
+SCALAR, VECTOR = "scalar", "vector"
 
 
 def tile_ensemblenet_pa_v_kernel(tc, d1_t, d1_f, xt, xf, W_gt, W_gf, b_g, z, dinv_t, grad_out, out_0, out_1):
@@ -37,93 +38,94 @@ def tile_ensemblenet_pa_v_kernel(tc, d1_t, d1_f, xt, xf, W_gt, W_gf, b_g, z, din
         def bank(number, name):
             return ps.tile([P, PASS], F32, name=name, tag="bank%d" % number)
 
-        pairs = [(g, c) for g in range(PASSES) for c in range(PASSES)]
-        dist = {(g, c, half): sbuf("dist%d%d%d" % (g, c, half), 2 * PASS, BF16) for g, c in pairs for half in range(2)}
-        root = {(g, c): sbuf("root%d%d" % (g, c), PACK * PASS, F32) for g, c in pairs}
-        adj = {(g, c): sbuf("adj%d%d" % (g, c), PACK * PASS, BF16) for g, c in pairs}
-        adj_codes = {(g, c): sbuf("adj_codes%d%d" % (g, c), PASS, U32) for g, c in pairs}
-        adj_scales = {(g, c): sbuf("adj_scales%d%d" % (g, c), PASS, U8) for g, c in pairs}
-        halves = [(g, half) for g in range(PASSES) for half in range(2)]
-        z_sb = {k: sbuf("z%d%d" % k, 2 * H, F32) for k in halves}
-        grad = [sbuf("grad%d" % g, PACK * H, BF16) for g in range(PASSES)]
-        gate = [sbuf("gate%d" % g, PACK * H, F32) for g in range(PASSES)]
-        dz2 = [sbuf("dz2_%d" % g, PACK * H, BF16) for g in range(PASSES)]
+        panels = [(g, c) for g in range(PASSES) for c in range(PASSES)]
+        pass_pairs = [(g, pair) for g in range(PASSES) for pair in range(2)]
+        root = {k: sbuf("root%d%d" % k, SLOTS * PASS, F32) for k in panels}
+        adj = {k: sbuf("adj%d%d" % k, SLOTS * PASS, BF16) for k in panels}
+        adj_codes = {k: sbuf("adj_codes%d%d" % k, PASS, U32) for k in panels}
+        adj_scales = {k: sbuf("adj_scales%d%d" % k, PASS, U8) for k in panels}
+        z_rows = {k: sbuf("z_rows%d%d" % k, 2 * H, F32) for k in pass_pairs}
+        grad = [sbuf("grad%d" % g, SLOTS * H, BF16) for g in range(PASSES)]
+        gate = [sbuf("gate%d" % g, SLOTS * H, F32) for g in range(PASSES)]
+        dz2 = [sbuf("dz2_%d" % g, SLOTS * H, BF16) for g in range(PASSES)]
         dz2_codes = [sbuf("dz2_codes%d" % g, H, U32) for g in range(PASSES)]
         dz2_scales = [sbuf("dz2_scales%d" % g, H, U8) for g in range(PASSES)]
-        dz1_rows = [sbuf("dz1_rows%d" % c, PACK * H, BF16) for c in range(PASSES)]
-        dz1_by_node = [sbuf("dz1_by_node%d" % c, PACK * H, BF16) for c in range(PASSES)]
+        dz1_rows = [sbuf("dz1_rows%d" % c, SLOTS * H, BF16) for c in range(PASSES)]
+        dz1_by_node = [sbuf("dz1_by_node%d" % c, SLOTS * H, BF16) for c in range(PASSES)]
         node_codes = [sbuf("node_codes%d" % c, H, U32) for c in range(PASSES)]
         node_scales = [sbuf("node_scales%d" % c, H, U8) for c in range(PASSES)]
-        dz1_by_feat = {k: sbuf("dz1_by_feat%d%d" % k, 2 * H, BF16) for k in halves}
-        feat_codes = {k: sbuf("feat_codes%d%d" % k, 2 * P, U32) for k in halves}
-        feat_scales = {k: sbuf("feat_scales%d%d" % k, 2 * P, U8) for k in halves}
-        x_rows = sbuf("x_rows", PASSES * PACK * D, BF16)
-        x_packed = sbuf("x_packed", PASSES * PACK * D, BF16)
+        dz1_by_feat = {k: sbuf("dz1_by_feat%d%d" % k, 2 * H, BF16) for k in pass_pairs}
+        feat_codes = {k: sbuf("feat_codes%d%d" % k, 2 * P, U32) for k in pass_pairs}
+        feat_scales = {k: sbuf("feat_scales%d%d" % k, 2 * P, U8) for k in pass_pairs}
+        x_rows = sbuf("x_rows", PASSES * SLOTS * D, BF16)
+        x_packed = sbuf("x_packed", PASSES * SLOTS * D, BF16)
         x_codes = sbuf("x_codes", PASSES * D, U32)
         x_scales = sbuf("x_scales", PASSES * D, U8)
         w_rows = sbuf("w_rows", H, BF16)
-        w_packed = sbuf("w_packed", PACK * D, BF16)
-        w_codes = sbuf("w_codes", (PACK + 1) * D, U32)
-        w_scales = sbuf("w_scales", (PACK + 1) * D, U8)
-        dinv = sbuf("dinv", PASSES * PACK, F32)
+        w_packed = sbuf("w_packed", SLOTS * D, BF16)
+        w_codes = sbuf("w_codes", PASS + D, U32)
+        w_scales = sbuf("w_scales", PASS + D, U8)
+        dinv = sbuf("dinv", PASSES * SLOTS, F32)
         ident = sbuf("ident", P, F32)
+        cap_line = sbuf("cap_line", SLOTS, F32)
         loop_cap = sbuf("loop_cap", PASS, F32)
-        warm = sbuf("warm", 8, F32)
-        cap_row = sbuf("cap_row", PACK, F32)
-        dx_sb = {k: sbuf("dx_sb%d%d" % k, 2 * D, F32) for k in halves}
-        dw_sb = sbuf("dw_sb", H, F32)
-        dh, flipped, dx_ps, dw_ps = {}, {}, {}, {}
+        dx_rows = {k: sbuf("dx_rows%d%d" % k, 2 * D, F32) for k in pass_pairs}
+        dw_cols = [sbuf("dw_cols%d" % half, H // 2, F32) for half in range(2)]
+        dist, dh, flipped, dx_sum, single = {}, {}, {}, {}, {}
 
-        def rows_of(src, g, half):
-            return src[g * PASS:(g + 1) * PASS, :].rearrange("(p t) w -> p t w", t=PACK)[:, 2 * half:2 * half + 2, :]
+        def pair_of_rows(tensor, g, pair):
+            rows = tensor[g * PASS:(g + 1) * PASS, :].rearrange("(p t) w -> p t w", t=SLOTS)
+            return rows[:, 2 * pair:2 * pair + 2, :]
 
-        def load_dist(g, c, half):
-            nc.sync.dma_start(out=dist[g, c, half][:].rearrange("p (t j) -> p t j", t=2),
-                              in_=rows_of(d1_t, g, half)[:, :, c * PASS:(c + 1) * PASS])
+        def load_dist(g, pair, c_first, c_end):
+            landed = sbuf("dist%d%d%d" % (g, pair, c_first), 2 * (c_end - c_first) * PASS, BF16)
+            rows = landed[:].rearrange("p (t j) -> p t j", t=2)
+            nc.sync.dma_start(out=rows, in_=pair_of_rows(d1_t, g, pair)[:, :, c_first * PASS:c_end * PASS])
+            for c in range(c_first, c_end):
+                dist[g, c, pair] = rows[:, :, (c - c_first) * PASS:(c - c_first + 1) * PASS]
 
-        def load_z(g, half):
-            nc.sync.dma_start(out=z_sb[g, half][:].rearrange("p (t h) -> p t h", t=2), in_=rows_of(z, g, half))
+        def load_z(g, pair):
+            nc.sync.dma_start(out=z_rows[g, pair][:].rearrange("p (t h) -> p t h", t=2), in_=pair_of_rows(z, g, pair))
 
         def load_grad(g):
-            nc.sync.dma_start(out=grad[g][:], in_=grad_out[g * PASS:(g + 1) * PASS, :].rearrange("(p t) h -> p (t h)", t=PACK))
+            nc.sync.dma_start(out=grad[g][:],
+                              in_=grad_out[g * PASS:(g + 1) * PASS, :].rearrange("(p t) h -> p (t h)", t=SLOTS))
 
         def load_dinv():
             nc.sync.dma_start(out=dinv[:].rearrange("p (g t) -> p g t", g=PASSES),
-                              in_=dinv_t.rearrange("(g p t) -> p g t", g=PASSES, t=PACK))
+                              in_=dinv_t.rearrange("(g p t) -> p g t", g=PASSES, t=SLOTS))
 
         def load_x():
             nc.sync.dma_start(out=x_rows[:].rearrange("p (c w) -> p c w", c=PASSES),
-                              in_=xt.rearrange("(c p s) d -> p c (s d)", c=PASSES, s=PACK))
+                              in_=xt.rearrange("(c p s) d -> p c (s d)", c=PASSES, s=SLOTS))
 
         def load_w():
             nc.sync.dma_start(out=w_rows[:], in_=W_gt)
 
         def constants():
             make_identity(nc, ident[:])
-            nc.vector.memset(warm[:], 1.0)
-            nc.scalar.activation(out=warm[:, 0:1], in_=warm[:, 0:1], func=ACT.Abs_reciprocal_sqrt)
-            nc.vector.memset(cap_row[:], CAP)
-            nc.vector.memset(cap_row[:, 1:3], 2 * CAP + 1)
+            nc.vector.memset(cap_line[:], CAP)
+            nc.scalar.activation(out=cap_line[:, 1:3], in_=cap_line[:, 1:3], func=ACT.Abs_reciprocal_sqrt, scale=2.0 ** -70)
             nc.vector.memset(w_codes[:], 0)
             nc.vector.memset(w_scales[:].bitcast(U32), 0)
-            nc.vector.scalar_tensor_tensor(out=loop_cap[:].rearrange("p (m q) -> p m q", q=PACK),
-                                           in0=ident[:].unsqueeze(2).to_broadcast([P, P, PACK]), scalar=-(CAP + 1),
-                                           in1=cap_row[:].unsqueeze(1).to_broadcast([P, P, PACK]),
+            nc.vector.scalar_tensor_tensor(out=loop_cap[:].rearrange("p (m q) -> p m q", q=SLOTS),
+                                           in0=ident[:].unsqueeze(2).to_broadcast([P, P, SLOTS]), scalar=-(CAP + 1),
+                                           in1=cap_line[:].unsqueeze(1).to_broadcast([P, P, SLOTS]),
                                            op0=ALU.mult, op1=ALU.add)
 
-        def inverse_root(g, c, half):
-            nc.scalar.activation(out=root[g, c][:, half * 2 * PASS:(half + 1) * 2 * PASS].rearrange("p (j t) -> p j t", t=2),
-                                 in_=dist[g, c, half][:].rearrange("p (t j) -> p j t", t=2),
+        def inverse_root(g, c, pair):
+            dst = root[g, c][:, pair * 2 * PASS:(pair + 1) * 2 * PASS].rearrange("p (j e) -> p j e", e=2)
+            nc.scalar.activation(out=dst, in_=dist[g, c, pair].rearrange("p e j -> p j e"),
                                  func=ACT.Abs_reciprocal_sqrt, bias=EPS)
 
-        def self_loops(g, half):
-            lines = root[g, g][:].rearrange("p (a m b q) -> p a b m q", a=2, b=2, q=PACK)[:, half, half]
-            nc.vector.tensor_tensor(out=lines, in0=lines, in1=loop_cap[:].rearrange("p (m q) -> p m q", q=PACK), op=ALU.min)
+        def self_loops(g, pair):
+            fours = root[g, g][:].rearrange("p (a m b q) -> p a b m q", a=2, b=2, q=SLOTS)[:, pair, pair]
+            nc.vector.tensor_tensor(out=fours, in0=fours, in1=loop_cap[:].rearrange("p (m q) -> p m q", q=SLOTS), op=ALU.min)
 
         def square(engine, g, c, s):
-            src = root[g, c][:].rearrange("p (a m s t) -> p s m a t", a=2, s=PACK, t=2)[:, s]
-            dst = adj[g, c][:, s * PASS:(s + 1) * PASS].rearrange("p (m a t) -> p m a t", a=2, t=2)
-            if engine == "scalar":
+            src = root[g, c][:].rearrange("p (a m s e) -> p s m a e", a=2, s=SLOTS, e=2)[:, s]
+            dst = adj[g, c][:, s * PASS:(s + 1) * PASS].rearrange("p (m a e) -> p m a e", a=2, e=2)
+            if engine == SCALAR:
                 nc.scalar.activation(out=dst, in_=src, func=ACT.Square)
             else:
                 nc.vector.tensor_tensor(out=dst, in0=src, in1=src, op=ALU.mult)
@@ -132,247 +134,227 @@ def tile_ensemblenet_pa_v_kernel(tc, d1_t, d1_f, xt, xf, W_gt, W_gf, b_g, z, din
             nc.vector.quantize_mx(out=codes[:, first:first + count].bitcast(fmt), scales=scales[:, first:first + count],
                                   in_=values)
 
-        def quantise_adj(g, c, s0, s1):
-            quantise(adj[g, c][:, s0 * PASS:s1 * PASS], adj_codes[g, c], adj_scales[g, c], E4M3, s0 * P, (s1 - s0) * P)
+        def quantise_adj(g, c, s_first, s_end):
+            quantise(adj[g, c][:, s_first * PASS:s_end * PASS], adj_codes[g, c], adj_scales[g, c], E4M3,
+                     s_first * P, (s_end - s_first) * P)
 
-        def interleave(dst, src):
-            nc.vector.tensor_copy(out=dst.rearrange("p (c i t) -> p c t i", i=4, t=PACK), in_=src)
-
-        def gate_rows(g, half):
-            for row in range(2):
-                t = 2 * half + row
-                nc.vector.tensor_scalar(out=gate[g][:, t * H:(t + 1) * H], in0=z_sb[g, half][:, row * H:(row + 1) * H],
-                                        scalar1=0.0, scalar2=dinv[:, g * PACK + t:g * PACK + t + 1],
+        def gate_rows(g, pair):
+            for e in range(2):
+                t = 2 * pair + e
+                nc.vector.tensor_scalar(out=gate[g][:, t * H:(t + 1) * H], in0=z_rows[g, pair][:, e * H:(e + 1) * H],
+                                        scalar1=0.0, scalar2=dinv[:, g * SLOTS + t:g * SLOTS + t + 1],
                                         op0=ALU.is_gt, op1=ALU.mult)
 
         def round_dz2(g, half):
             order = "p (t k c i) -> p k c t i"
-            nc.vector.tensor_tensor(out=dz2[g][:, half * 2 * H:(half + 1) * 2 * H].rearrange("p (c i t) -> p c t i", i=2, t=PACK),
-                                    in0=gate[g][:].rearrange(order, t=PACK, k=2, i=2)[:, half],
-                                    in1=grad[g][:].rearrange(order, t=PACK, k=2, i=2)[:, half], op=ALU.mult)
+            dst = dz2[g][:, half * 2 * H:(half + 1) * 2 * H].rearrange("p (c i t) -> p c t i", i=2, t=SLOTS)
+            nc.vector.tensor_tensor(out=dst, in0=gate[g][:].rearrange(order, t=SLOTS, k=2, i=2)[:, half],
+                                    in1=grad[g][:].rearrange(order, t=SLOTS, k=2, i=2)[:, half], op=ALU.mult)
 
         def quantise_dz2(g):
             quantise(dz2[g][:], dz2_codes[g], dz2_scales[g], E5M2, 0, H)
 
-        def dh_pass(g, c, s, first):
-            if first:
-                dh[c, s] = bank(PACK * c + s, "dh%d%d" % (c, s))
+        def dh_pass(g, c, s):
+            if g == 0:
+                dh[c, s] = bank(SLOTS * c + s, "dh%d%d" % (c, s))
             cols = slice(s * P, (s + 1) * P)
             nc.tensor.matmul_mx(out=dh[c, s][:], lhsT=adj_codes[g, c][:, cols].bitcast(E4M3), lhsT_scale=adj_scales[g, c][:, cols],
-                                rhs=dz2_codes[g][:].bitcast(E5M2), rhs_scale=dz2_scales[g][:], start=first, stop=not first)
+                                rhs=dz2_codes[g][:].bitcast(E5M2), rhs_scale=dz2_scales[g][:],
+                                start=(g == 0), stop=(g == PASSES - 1))
 
         def round_dz1(engine, c, s):
             src = dh[c, s][:].rearrange("p (w u e) -> p u w e", u=2, e=2)
             dst = dz1_rows[c][:, s * H:(s + 1) * H].rearrange("p (u w e) -> p u w e", u=2, e=2)
-            factor = dinv[:, c * PACK + s:c * PACK + s + 1]
-            if engine == "scalar":
+            factor = dinv[:, c * SLOTS + s:c * SLOTS + s + 1]
+            if engine == SCALAR:
                 nc.scalar.activation(out=dst, in_=src, func=ACT.Copy, scale=factor)
             else:
                 nc.vector.tensor_scalar(out=dst, in0=src, scalar1=factor, scalar2=None, op0=ALU.mult)
 
-        def flip_dz1(c, s):
-            half, row = divmod(s, 2)
-            if (c, half) not in flipped:
-                flipped[c, half] = bank(PACK * c + 2 * half, "flipped%d%d" % (c, half))
-            words = dz1_rows[c][:, s * H:(s + 1) * H].bitcast(F32)
-            for u in range(2):
-                at = (2 * row + u) * P
-                nc.tensor.transpose(flipped[c, half][:, at:at + P], words[:, u * P:(u + 1) * P], ident[:])
+        def flip_dz1(c, pair):
+            flipped[c, pair] = bank(SLOTS * c + 2 * pair, "flipped%d%d" % (c, pair))
+            words = dz1_rows[c][:, pair * 2 * H:(pair + 1) * 2 * H].bitcast(F32)
+            for block in range(SLOTS):
+                cols = slice(block * P, (block + 1) * P)
+                nc.tensor.transpose(flipped[c, pair][:, cols], words[:, cols], ident[:])
 
         def copy(engine, dst, src):
-            if engine == "scalar":
+            if engine == SCALAR:
                 nc.scalar.copy(out=dst, in_=src)
             else:
                 nc.vector.tensor_copy(out=dst, in_=src)
 
-        def pack_feat(engine, c, half):
-            copy(engine, dz1_by_feat[c, half][:].bitcast(F32).rearrange("p (s m u) -> p s m u", s=2, u=2),
-                 flipped[c, half][:].rearrange("p (s u m) -> p s m u", s=2, u=2))
+        def pack_feat(c, pair):
+            copy(SCALAR, dz1_by_feat[c, pair][:].bitcast(F32).rearrange("p (e m u) -> p e m u", e=2, u=2),
+                 flipped[c, pair][:].rearrange("p (e u m) -> p e m u", e=2, u=2))
 
-        def quantise_feat(c, half):
-            quantise(dz1_by_feat[c, half][:], feat_codes[c, half], feat_scales[c, half], E5M2, 0, 2 * P)
+        def quantise_feat(c, pair):
+            quantise(dz1_by_feat[c, pair][:], feat_codes[c, pair], feat_scales[c, pair], E5M2, 0, 2 * P)
 
-        def dx_pass(c, s):
-            half, row = divmod(s, 2)
-            if row == 0:
-                dx_ps[c, half] = bank(PACK * c + 2 * half + 1, "dx%d%d" % (c, half))
-            cols = slice(row * P, (row + 1) * P)
-            window = slice((1 - row) * D, (1 - row + PACK) * D)
-            nc.tensor.matmul_mx(out=dx_ps[c, half][:], lhsT=feat_codes[c, half][:, cols].bitcast(E5M2), lhsT_scale=feat_scales[c, half][:, cols],
-                                rhs=w_codes[:, window].bitcast(E4M3), rhs_scale=w_scales[:, window],
-                                start=(row == 0), stop=(row == 1))
+        def dx_passes(c, pair):
+            dx_sum[c, pair] = bank(SLOTS * c + 2 * pair + 1, "dx_sum%d%d" % (c, pair))
+            for e in range(2):
+                cols = slice(e * P, (e + 1) * P)
+                window = slice((1 - e) * D, (1 - e) * D + PASS)
+                nc.tensor.matmul_mx(out=dx_sum[c, pair][:], lhsT=feat_codes[c, pair][:, cols].bitcast(E5M2),
+                                    lhsT_scale=feat_scales[c, pair][:, cols],
+                                    rhs=w_codes[:, window].bitcast(E4M3), rhs_scale=w_scales[:, window],
+                                    start=(e == 0), stop=(e == 1))
 
-        def store_dx(engine, c, half):
-            copy(engine, dx_sb[c, half][:], dx_ps[c, half][:, 0:2 * D])
-            nc.sync.dma_start(out=rows_of(out_0, c, half), in_=dx_sb[c, half][:].rearrange("p (s d) -> p s d", s=2))
+        def store_dx(c, pair, queue):
+            copy(SCALAR, dx_rows[c, pair][:], dx_sum[c, pair][:, 0:2 * D])
+            queue.dma_start(out=pair_of_rows(out_0, c, pair), in_=dx_rows[c, pair][:].rearrange("p (e d) -> p e d", e=2))
 
         def pack_node(c, half):
-            src = dz1_rows[c][:].rearrange("p (s k c i) -> p k c s i", s=PACK, k=2, i=4)[:, half]
-            interleave(dz1_by_node[c][:, half * 2 * H:(half + 1) * 2 * H], src)
+            src = dz1_rows[c][:].rearrange("p (s k n i) -> p k n s i", s=SLOTS, k=2, i=4)[:, half]
+            dst = dz1_by_node[c][:, half * 2 * H:(half + 1) * 2 * H].rearrange("p (n i s) -> p n s i", i=4, s=SLOTS)
+            nc.vector.tensor_copy(out=dst, in_=src)
 
         def quantise_node(c, half):
-            quantise(dz1_by_node[c][:, half * 2 * H:(half + 1) * 2 * H], node_codes[c], node_scales[c], E5M2, half * 2 * P, 2 * P)
+            quantise(dz1_by_node[c][:, half * 2 * H:(half + 1) * 2 * H], node_codes[c], node_scales[c], E5M2,
+                     half * H // 2, H // 2)
 
         def dw_pass(c, first):
             if first:
-                dw_ps[0] = bank(PACK * c, "dw")
+                single["dw"] = bank(SLOTS * c, "dw_sum")
             cols = slice(c * D, (c + 1) * D)
-            nc.tensor.matmul_mx(out=dw_ps[0][:], lhsT=x_codes[:, cols].bitcast(E4M3), lhsT_scale=x_scales[:, cols],
+            nc.tensor.matmul_mx(out=single["dw"][:], lhsT=x_codes[:, cols].bitcast(E4M3), lhsT_scale=x_scales[:, cols],
                                 rhs=node_codes[c][:].bitcast(E5M2), rhs_scale=node_scales[c][:],
                                 start=first, stop=not first)
 
-        def store_dw(engine):
-            copy(engine, dw_sb[:].rearrange("p (w u e) -> p w u e", u=2, e=2),
-                 dw_ps[0][:].rearrange("p (u w e) -> p w u e", u=2, e=2))
-            nc.sync.dma_start(out=out_1, in_=dw_sb[:])
+        def store_dw():
+            for half in range(2):
+                copy(VECTOR, dw_cols[half][:].rearrange("p (w u e) -> p w u e", u=2, e=2),
+                     single["dw"][:].rearrange("p (u k w e) -> p k w u e", u=2, k=2, e=2)[:, half])
+                nc.sync.dma_start(out=out_1[:, half * H // 2:(half + 1) * H // 2], in_=dw_cols[half][:])
 
         def pack_x():
-            nc.vector.tensor_copy(out=x_packed[:].rearrange("p (c k i s) -> p c k s i", c=PASSES, i=4, s=PACK),
-                                  in_=x_rows[:].rearrange("p (c s k i) -> p c k s i", c=PASSES, s=PACK, i=4))
+            nc.vector.tensor_copy(out=x_packed[:].rearrange("p (c n i s) -> p c n s i", c=PASSES, i=4, s=SLOTS),
+                                  in_=x_rows[:].rearrange("p (c s n i) -> p c n s i", c=PASSES, s=SLOTS, i=4))
 
         def quantise_x():
             quantise(x_packed[:], x_codes, x_scales, E4M3, 0, PASSES * D)
 
         def flip_w():
-            flipped["w"] = bank(2 * PACK - 2, "flipped_w")
+            single["w"] = bank(SLOTS + 2, "flipped_w")
             words = w_rows[:].bitcast(F32)
             for u in range(2):
-                nc.tensor.transpose(flipped["w"][:, u * P:(u + 1) * P], words[:, u:2 * P:2], ident[:])
+                nc.tensor.transpose(single["w"][:, u * P:(u + 1) * P], words[:, u:2 * P:2], ident[:])
 
-        def pack_w(engine):
-            copy(engine, w_packed[:].bitcast(F32).rearrange("p (d u) -> p d u", u=2),
-                 flipped["w"][:, 0:2 * P].rearrange("p (u d) -> p d u", u=2))
+        def pack_w():
+            copy(VECTOR, w_packed[:].bitcast(F32).rearrange("p (d u) -> p d u", u=2),
+                 single["w"][:, 0:2 * P].rearrange("p (u d) -> p d u", u=2))
 
         def quantise_w():
             quantise(w_packed[:], w_codes, w_scales, E4M3, D, D)
 
-        S, V = "scalar", "vector"
-        load_dist(0, 0, 0)
+        load_dist(0, 0, 0, 1)
         constants()
-        load_dist(0, 0, 1)
+        load_dist(0, 1, 0, 1)
         load_dinv()
-        load_dist(1, 1, 0)
-        load_z(0, 0)
-        load_z(0, 1)
-        load_dist(0, 1, 0)
-        load_dist(0, 1, 1)
+        load_dist(1, 0, 0, PASSES)
+        for pair in range(2):
+            load_z(0, pair)
         load_grad(0)
-        load_dist(1, 1, 1)
-        load_z(1, 0)
-        load_z(1, 1)
+        for pair in range(2):
+            load_dist(0, pair, 1, PASSES)
+        load_dist(1, 1, 0, PASSES)
+        for pair in range(2):
+            load_z(1, pair)
         load_w()
         load_grad(1)
-        load_dist(1, 0, 0)
-        load_dist(1, 0, 1)
         load_x()
-        inverse_root(0, 0, 0)
-        inverse_root(0, 0, 1)
+
+        for pair in range(2):
+            inverse_root(0, 0, pair)
         inverse_root(1, 1, 0)
-        self_loops(0, 0)
-        self_loops(0, 1)
+        for pair in range(2):
+            self_loops(0, pair)
         gate_rows(0, 0)
-        square(S, 0, 0, 0)
-        square(S, 0, 0, 1)
-        square(V, 0, 0, 2)
+        for s in range(2):
+            square(SCALAR, 0, 0, s)
+        square(VECTOR, 0, 0, 3)
         gate_rows(0, 1)
-        square(V, 0, 0, 3)
         self_loops(1, 0)
-        quantise_adj(0, 0, 0, 4)
-        inverse_root(0, 1, 0)
-        inverse_root(0, 1, 1)
-        inverse_root(1, 1, 1)
-        square(S, 0, 1, 0)
-        square(S, 0, 1, 1)
-        square(S, 0, 1, 2)
-        square(S, 0, 1, 3)
-        round_dz2(0, 0)
-        round_dz2(0, 1)
-        self_loops(1, 1)
-        quantise_dz2(0)
-        gate_rows(1, 0)
-        gate_rows(1, 1)
-        quantise_adj(0, 1, 0, 4)
-        square(S, 1, 1, 0)
-        square(S, 1, 1, 1)
-        square(S, 1, 1, 2)
-        square(S, 1, 1, 3)
-        flip_w()
-        dh_pass(0, 0, 0, True)
-        dh_pass(0, 0, 1, True)
-        dh_pass(0, 0, 2, True)
-        dh_pass(0, 0, 3, True)
-        round_dz2(1, 0)
-        round_dz2(1, 1)
-        pack_w(V)
-        quantise_dz2(1)
-        quantise_adj(1, 1, 0, 4)
-        dh_pass(0, 1, 0, True)
-        dh_pass(0, 1, 1, True)
-        dh_pass(0, 1, 2, True)
-        dh_pass(0, 1, 3, True)
         inverse_root(1, 0, 0)
+        square(SCALAR, 0, 0, 2)
+        for half in range(2):
+            round_dz2(0, half)
+        quantise_adj(0, 0, 0, SLOTS)
+        quantise_dz2(0)
+
+        for pair in range(2):
+            inverse_root(0, 1, pair)
+        inverse_root(1, 1, 1)
+        square(VECTOR, 0, 1, 3)
+        for s in range(SLOTS - 1):
+            square(SCALAR, 0, 1, s)
+        gate_rows(1, 0)
+        self_loops(1, 1)
+        gate_rows(1, 1)
+        quantise_adj(0, 1, 0, SLOTS)
+        for s in range(SLOTS):
+            square(SCALAR, 1, 1, s)
         inverse_root(1, 0, 1)
-        dh_pass(1, 1, 0, False)
-        dh_pass(1, 1, 1, False)
-        dh_pass(1, 1, 2, False)
-        dh_pass(1, 1, 3, False)
-        square(S, 1, 0, 0)
-        square(S, 1, 0, 1)
+        flip_w()
+        for s in range(SLOTS):
+            dh_pass(0, 0, s)
+        for half in range(2):
+            round_dz2(1, half)
+        pack_w()
+        quantise_dz2(1)
+        quantise_adj(1, 1, 0, SLOTS)
+        for g in range(PASSES):
+            for s in range(SLOTS):
+                dh_pass(g, 1, s)
+
+        for s in range(SLOTS):
+            square(SCALAR, 1, 0, s)
         pack_x()
-        square(V, 1, 0, 2)
         quantise_w()
-        square(S, 1, 0, 3)
         quantise_x()
         quantise_adj(1, 0, 0, 2)
-        round_dz1(V, 1, 0)
-        quantise_adj(1, 0, 2, 4)
-        round_dz1(S, 1, 1)
-        round_dz1(S, 1, 2)
-        round_dz1(V, 1, 3)
-        dh_pass(1, 0, 0, False)
-        dh_pass(1, 0, 1, False)
-        flip_dz1(1, 0)
-        flip_dz1(1, 1)
-        dh_pass(1, 0, 2, False)
-        dh_pass(1, 0, 3, False)
-        flip_dz1(1, 2)
-        flip_dz1(1, 3)
-        round_dz1(S, 0, 0)
-        round_dz1(S, 0, 1)
-        pack_feat(S, 1, 0)
-        round_dz1(S, 0, 2)
-        round_dz1(S, 0, 3)
-        pack_node(1, 0)
-        pack_node(1, 1)
+        round_dz1(VECTOR, 1, 0)
+        quantise_adj(1, 0, 2, SLOTS)
+        for s in range(1, SLOTS - 1):
+            round_dz1(SCALAR, 1, s)
+        round_dz1(VECTOR, 1, SLOTS - 1)
+        for pair in range(2):
+            for s in range(2 * pair, 2 * pair + 2):
+                dh_pass(1, 0, s)
+            flip_dz1(1, pair)
+
+        for s in range(2):
+            round_dz1(SCALAR, 0, s)
+        pack_feat(1, 0)
+        for s in range(2, SLOTS):
+            round_dz1(SCALAR, 0, s)
+        for half in range(2):
+            pack_node(1, half)
         quantise_feat(1, 0)
-        quantise_node(1, 0)
-        quantise_node(1, 1)
+        for half in range(2):
+            quantise_node(1, half)
         flip_dz1(0, 0)
+        dx_passes(1, 0)
         flip_dz1(0, 1)
-        dx_pass(1, 0)
-        dx_pass(1, 1)
-        flip_dz1(0, 2)
-        flip_dz1(0, 3)
         dw_pass(1, True)
-        pack_feat(S, 0, 0)
-        pack_feat(S, 1, 1)
-        pack_feat(S, 0, 1)
+        pack_feat(0, 0)
+        pack_feat(1, 1)
+        pack_feat(0, 1)
         pack_node(0, 0)
         quantise_feat(0, 0)
         pack_node(0, 1)
         quantise_feat(1, 1)
-        quantise_node(0, 0)
-        quantise_node(0, 1)
+        for half in range(2):
+            quantise_node(0, half)
         quantise_feat(0, 1)
-        dx_pass(0, 0)
-        dx_pass(0, 1)
-        dx_pass(1, 2)
-        dx_pass(1, 3)
+        dx_passes(0, 0)
+        dx_passes(1, 1)
         dw_pass(0, False)
-        dx_pass(0, 2)
-        dx_pass(0, 3)
-        store_dx(S, 1, 0)
-        store_dx(S, 0, 0)
-        store_dx(S, 1, 1)
-        store_dw(V)
-        store_dx(S, 0, 1)
+        dx_passes(0, 1)
+
+        store_dx(1, 0, nc.sync)
+        store_dx(0, 0, nc.sync)
+        store_dx(1, 1, nc.sync)
+        store_dw()
+        store_dx(0, 1, nc.scalar)

@@ -40,6 +40,7 @@ def tile_ensemblenet_pa_v_kernel(tc, d1_t, d1_f, xt, xf, W_gt, W_gf, b_g, z, din
 
         panels = [(g, c) for g in range(PASSES) for c in range(PASSES)]
         pass_pairs = [(g, pair) for g in range(PASSES) for pair in range(2)]
+        dist = {(g, c, pair): sbuf("dist%d%d%d" % (g, c, pair), 2 * PASS, BF16) for g, c in panels for pair in range(2)}
         root = {k: sbuf("root%d%d" % k, SLOTS * PASS, F32) for k in panels}
         adj = {k: sbuf("adj%d%d" % k, SLOTS * PASS, BF16) for k in panels}
         adj_codes = {k: sbuf("adj_codes%d%d" % k, PASS, U32) for k in panels}
@@ -70,22 +71,19 @@ def tile_ensemblenet_pa_v_kernel(tc, d1_t, d1_f, xt, xf, W_gt, W_gf, b_g, z, din
         cap_line = sbuf("cap_line", SLOTS, F32)
         loop_cap = sbuf("loop_cap", PASS, F32)
         dx_rows = {k: sbuf("dx_rows%d%d" % k, 2 * D, F32) for k in pass_pairs}
-        dw_cols = [sbuf("dw_cols%d" % half, H // 2, F32) for half in range(2)]
-        dist, dh, flipped, dx_sum, single = {}, {}, {}, {}, {}
+        dw_rows = sbuf("dw_rows", H, F32)
+        dh, flipped, dx_sum, single = {}, {}, {}, {}
 
         def pair_of_rows(tensor, g, pair):
             rows = tensor[g * PASS:(g + 1) * PASS, :].rearrange("(p t) w -> p t w", t=SLOTS)
             return rows[:, 2 * pair:2 * pair + 2, :]
 
-        def load_dist(g, pair, c_first, c_end):
-            landed = sbuf("dist%d%d%d" % (g, pair, c_first), 2 * (c_end - c_first) * PASS, BF16)
-            rows = landed[:].rearrange("p (t j) -> p t j", t=2)
-            nc.sync.dma_start(out=rows, in_=pair_of_rows(d1_t, g, pair)[:, :, c_first * PASS:c_end * PASS])
-            for c in range(c_first, c_end):
-                dist[g, c, pair] = rows[:, :, (c - c_first) * PASS:(c - c_first + 1) * PASS]
+        def load_dist(g, c, pair):
+            nc.sync.dma_start(out=dist[g, c, pair][:].rearrange("p (e j) -> p e j", e=2),
+                              in_=pair_of_rows(d1_t, g, pair)[:, :, c * PASS:(c + 1) * PASS])
 
         def load_z(g, pair):
-            nc.sync.dma_start(out=z_rows[g, pair][:].rearrange("p (t h) -> p t h", t=2), in_=pair_of_rows(z, g, pair))
+            nc.sync.dma_start(out=z_rows[g, pair][:].rearrange("p (e h) -> p e h", e=2), in_=pair_of_rows(z, g, pair))
 
         def load_grad(g):
             nc.sync.dma_start(out=grad[g][:],
@@ -115,7 +113,7 @@ def tile_ensemblenet_pa_v_kernel(tc, d1_t, d1_f, xt, xf, W_gt, W_gf, b_g, z, din
 
         def inverse_root(g, c, pair):
             dst = root[g, c][:, pair * 2 * PASS:(pair + 1) * 2 * PASS].rearrange("p (j e) -> p j e", e=2)
-            nc.scalar.activation(out=dst, in_=dist[g, c, pair].rearrange("p e j -> p j e"),
+            nc.scalar.activation(out=dst, in_=dist[g, c, pair][:].rearrange("p (e j) -> p j e", e=2),
                                  func=ACT.Abs_reciprocal_sqrt, bias=EPS)
 
         def self_loops(g, pair):
@@ -201,9 +199,9 @@ def tile_ensemblenet_pa_v_kernel(tc, d1_t, d1_f, xt, xf, W_gt, W_gf, b_g, z, din
                                     rhs=w_codes[:, window].bitcast(E4M3), rhs_scale=w_scales[:, window],
                                     start=(e == 0), stop=(e == 1))
 
-        def store_dx(c, pair, queue):
+        def store_dx(c, pair):
             copy(SCALAR, dx_rows[c, pair][:], dx_sum[c, pair][:, 0:2 * D])
-            queue.dma_start(out=pair_of_rows(out_0, c, pair), in_=dx_rows[c, pair][:].rearrange("p (e d) -> p e d", e=2))
+            nc.sync.dma_start(out=pair_of_rows(out_0, c, pair), in_=dx_rows[c, pair][:].rearrange("p (e d) -> p e d", e=2))
 
         def pack_node(c, half):
             src = dz1_rows[c][:].rearrange("p (s k n i) -> p k n s i", s=SLOTS, k=2, i=4)[:, half]
@@ -223,10 +221,9 @@ def tile_ensemblenet_pa_v_kernel(tc, d1_t, d1_f, xt, xf, W_gt, W_gf, b_g, z, din
                                 start=first, stop=not first)
 
         def store_dw():
-            for half in range(2):
-                copy(VECTOR, dw_cols[half][:].rearrange("p (w u e) -> p w u e", u=2, e=2),
-                     single["dw"][:].rearrange("p (u k w e) -> p k w u e", u=2, k=2, e=2)[:, half])
-                nc.sync.dma_start(out=out_1[:, half * H // 2:(half + 1) * H // 2], in_=dw_cols[half][:])
+            copy(VECTOR, dw_rows[:].rearrange("p (w u e) -> p w u e", u=2, e=2),
+                 single["dw"][:].rearrange("p (u w e) -> p w u e", u=2, e=2))
+            nc.sync.dma_start(out=out_1, in_=dw_rows[:])
 
         def pack_x():
             nc.vector.tensor_copy(out=x_packed[:].rearrange("p (c n i s) -> p c n s i", c=PASSES, i=4, s=SLOTS),
@@ -248,21 +245,23 @@ def tile_ensemblenet_pa_v_kernel(tc, d1_t, d1_f, xt, xf, W_gt, W_gf, b_g, z, din
         def quantise_w():
             quantise(w_packed[:], w_codes, w_scales, E4M3, D, D)
 
-        load_dist(0, 0, 0, 1)
+        load_dist(0, 0, 0)
         constants()
-        load_dist(0, 1, 0, 1)
+        load_dist(0, 0, 1)
         load_dinv()
-        load_dist(1, 0, 0, PASSES)
+        load_dist(1, 1, 0)
         for pair in range(2):
             load_z(0, pair)
-        load_grad(0)
         for pair in range(2):
-            load_dist(0, pair, 1, PASSES)
-        load_dist(1, 1, 0, PASSES)
+            load_dist(0, 1, pair)
+        load_grad(0)
+        load_dist(1, 1, 1)
         for pair in range(2):
             load_z(1, pair)
         load_w()
         load_grad(1)
+        for pair in range(2):
+            load_dist(1, 0, pair)
         load_x()
 
         for pair in range(2):
@@ -270,32 +269,27 @@ def tile_ensemblenet_pa_v_kernel(tc, d1_t, d1_f, xt, xf, W_gt, W_gf, b_g, z, din
         inverse_root(1, 1, 0)
         for pair in range(2):
             self_loops(0, pair)
-        gate_rows(0, 0)
-        for s in range(2):
-            square(SCALAR, 0, 0, s)
-        square(VECTOR, 0, 0, 3)
-        gate_rows(0, 1)
+        for pair in range(2):
+            gate_rows(0, pair)
+            square(SCALAR, 0, 0, pair)
+            square(VECTOR, 0, 0, 2 + pair)
         self_loops(1, 0)
-        inverse_root(1, 0, 0)
-        square(SCALAR, 0, 0, 2)
-        for half in range(2):
-            round_dz2(0, half)
         quantise_adj(0, 0, 0, SLOTS)
-        quantise_dz2(0)
 
         for pair in range(2):
             inverse_root(0, 1, pair)
         inverse_root(1, 1, 1)
-        square(VECTOR, 0, 1, 3)
-        for s in range(SLOTS - 1):
+        for s in range(SLOTS):
             square(SCALAR, 0, 1, s)
-        gate_rows(1, 0)
+        for half in range(2):
+            round_dz2(0, half)
         self_loops(1, 1)
-        gate_rows(1, 1)
+        quantise_dz2(0)
+        for pair in range(2):
+            gate_rows(1, pair)
         quantise_adj(0, 1, 0, SLOTS)
         for s in range(SLOTS):
             square(SCALAR, 1, 1, s)
-        inverse_root(1, 0, 1)
         flip_w()
         for s in range(SLOTS):
             dh_pass(0, 0, s)
@@ -308,9 +302,12 @@ def tile_ensemblenet_pa_v_kernel(tc, d1_t, d1_f, xt, xf, W_gt, W_gf, b_g, z, din
             for s in range(SLOTS):
                 dh_pass(g, 1, s)
 
-        for s in range(SLOTS):
+        for pair in range(2):
+            inverse_root(1, 0, pair)
+        for s in (0, 1, 3):
             square(SCALAR, 1, 0, s)
         pack_x()
+        square(VECTOR, 1, 0, 2)
         quantise_w()
         quantise_x()
         quantise_adj(1, 0, 0, 2)
@@ -353,8 +350,8 @@ def tile_ensemblenet_pa_v_kernel(tc, d1_t, d1_f, xt, xf, W_gt, W_gf, b_g, z, din
         dw_pass(0, False)
         dx_passes(0, 1)
 
-        store_dx(1, 0, nc.sync)
-        store_dx(0, 0, nc.sync)
-        store_dx(1, 1, nc.sync)
+        store_dx(1, 0)
+        store_dx(0, 0)
+        store_dx(1, 1)
         store_dw()
-        store_dx(0, 1, nc.scalar)
+        store_dx(0, 1)

from contextlib import ExitStack

import concourse.mybir as mybir
from concourse.masks import make_identity

N, D, H = 1024, 128, 512
EPS = 1e-5
FLOPS = 2 * N * N * H + 2 * N * H * D + 2 * N * D * H
BYTES = 2 * (N * N + N * D + D * H + N * H) + 4 * (N * H + N + N * D + D * H)

F32 = mybir.dt.float32
BF16 = mybir.dt.bfloat16
U32 = mybir.dt.uint32
U8 = mybir.dt.uint8
E4M3 = mybir.dt.float8_e4m3fn_x4
E5M2 = mybir.dt.float8_e5m2_x4
ACT = mybir.ActivationFunctionType
ALU = mybir.AluOpType

P = 128
SLOTS = 4
PASS = P * SLOTS
PASSES = N // PASS
CAP = 2.0 ** 22
SCALAR, VECTOR = "scalar", "vector"


def tile_ensemblenet_pa_v_kernel(tc, d1_t, d1_f, xt, xf, W_gt, W_gf, b_g, z, dinv_t, grad_out, out_0, out_1):
    nc = tc.nc
    with ExitStack() as ctx:
        sb = ctx.enter_context(tc.tile_pool(name="sb", bufs=1))
        ps = ctx.enter_context(tc.psum_pool(name="ps", bufs=1))
        ctx.enter_context(tc.manual_schedule())

        def sbuf(name, width, dtype):
            return sb.tile([P, width], dtype, name=name, align_bytes=64)

        def bank(number, name):
            return ps.tile([P, PASS], F32, name=name, tag="bank%d" % number)

        panels = [(g, c) for g in range(PASSES) for c in range(PASSES)]
        pass_pairs = [(g, pair) for g in range(PASSES) for pair in range(2)]
        dist = {(g, c, pair): sbuf("dist%d%d%d" % (g, c, pair), 2 * PASS, BF16) for g, c in panels for pair in range(2)}
        root = {k: sbuf("root%d%d" % k, SLOTS * PASS, F32) for k in panels}
        adj = {k: sbuf("adj%d%d" % k, SLOTS * PASS, BF16) for k in panels}
        adj_codes = {k: sbuf("adj_codes%d%d" % k, PASS, U32) for k in panels}
        adj_scales = {k: sbuf("adj_scales%d%d" % k, PASS, U8) for k in panels}
        z_rows = {k: sbuf("z_rows%d%d" % k, 2 * H, F32) for k in pass_pairs}
        grad = [sbuf("grad%d" % g, SLOTS * H, BF16) for g in range(PASSES)]
        gate = [sbuf("gate%d" % g, SLOTS * H, F32) for g in range(PASSES)]
        dz2 = [sbuf("dz2_%d" % g, SLOTS * H, BF16) for g in range(PASSES)]
        dz2_codes = [sbuf("dz2_codes%d" % g, H, U32) for g in range(PASSES)]
        dz2_scales = [sbuf("dz2_scales%d" % g, H, U8) for g in range(PASSES)]
        dz1_rows = [sbuf("dz1_rows%d" % c, SLOTS * H, BF16) for c in range(PASSES)]
        dz1_by_node = [sbuf("dz1_by_node%d" % c, SLOTS * H, BF16) for c in range(PASSES)]
        node_codes = [sbuf("node_codes%d" % c, H, U32) for c in range(PASSES)]
        node_scales = [sbuf("node_scales%d" % c, H, U8) for c in range(PASSES)]
        dz1_by_feat = {k: sbuf("dz1_by_feat%d%d" % k, 2 * H, BF16) for k in pass_pairs}
        feat_codes = {k: sbuf("feat_codes%d%d" % k, 2 * P, U32) for k in pass_pairs}
        feat_scales = {k: sbuf("feat_scales%d%d" % k, 2 * P, U8) for k in pass_pairs}
        x_rows = sbuf("x_rows", PASSES * SLOTS * D, BF16)
        x_packed = sbuf("x_packed", PASSES * SLOTS * D, BF16)
        x_codes = sbuf("x_codes", PASSES * D, U32)
        x_scales = sbuf("x_scales", PASSES * D, U8)
        w_rows = sbuf("w_rows", H, BF16)
        w_packed = sbuf("w_packed", SLOTS * D, BF16)
        w_codes = sbuf("w_codes", PASS + D, U32)
        w_scales = sbuf("w_scales", PASS + D, U8)
        dinv = sbuf("dinv", PASSES * SLOTS, F32)
        ident = sbuf("ident", P, F32)
        cap_line = sbuf("cap_line", SLOTS, F32)
        loop_cap = sbuf("loop_cap", PASS, F32)
        dx_rows = {k: sbuf("dx_rows%d%d" % k, 2 * D, F32) for k in pass_pairs}
        dw_rows = sbuf("dw_rows", H, F32)
        dh, flipped, dx_sum, single = {}, {}, {}, {}

        def pair_of_rows(tensor, g, pair):
            rows = tensor[g * PASS:(g + 1) * PASS, :].rearrange("(p t) w -> p t w", t=SLOTS)
            return rows[:, 2 * pair:2 * pair + 2, :]

        def load_dist(g, c, pair):
            nc.sync.dma_start(out=dist[g, c, pair][:].rearrange("p (e j) -> p e j", e=2),
                              in_=pair_of_rows(d1_t, g, pair)[:, :, c * PASS:(c + 1) * PASS])

        def load_z(g, pair):
            nc.sync.dma_start(out=z_rows[g, pair][:].rearrange("p (e h) -> p e h", e=2), in_=pair_of_rows(z, g, pair))

        def load_grad(g):
            nc.sync.dma_start(out=grad[g][:],
                              in_=grad_out[g * PASS:(g + 1) * PASS, :].rearrange("(p t) h -> p (t h)", t=SLOTS))

        def load_dinv():
            nc.sync.dma_start(out=dinv[:].rearrange("p (g t) -> p g t", g=PASSES),
                              in_=dinv_t.rearrange("(g p t) -> p g t", g=PASSES, t=SLOTS))

        def load_x():
            nc.sync.dma_start(out=x_rows[:].rearrange("p (c w) -> p c w", c=PASSES),
                              in_=xt.rearrange("(c p s) d -> p c (s d)", c=PASSES, s=SLOTS))

        def load_w():
            nc.sync.dma_start(out=w_rows[:], in_=W_gt)

        def constants():
            make_identity(nc, ident[:])
            nc.vector.memset(cap_line[:], CAP)
            nc.scalar.activation(out=cap_line[:, 1:3], in_=cap_line[:, 1:3], func=ACT.Abs_reciprocal_sqrt, scale=2.0 ** -70)
            nc.vector.memset(w_codes[:], 0)
            nc.vector.memset(w_scales[:].bitcast(U32), 0)
            nc.vector.scalar_tensor_tensor(out=loop_cap[:].rearrange("p (m q) -> p m q", q=SLOTS),
                                           in0=ident[:].unsqueeze(2).to_broadcast([P, P, SLOTS]), scalar=-(CAP + 1),
                                           in1=cap_line[:].unsqueeze(1).to_broadcast([P, P, SLOTS]),
                                           op0=ALU.mult, op1=ALU.add)

        def inverse_root(g, c, pair):
            dst = root[g, c][:, pair * 2 * PASS:(pair + 1) * 2 * PASS].rearrange("p (j e) -> p j e", e=2)
            nc.scalar.activation(out=dst, in_=dist[g, c, pair][:].rearrange("p (e j) -> p j e", e=2),
                                 func=ACT.Abs_reciprocal_sqrt, bias=EPS)

        def self_loops(g, pair):
            fours = root[g, g][:].rearrange("p (a m b q) -> p a b m q", a=2, b=2, q=SLOTS)[:, pair, pair]
            nc.vector.tensor_tensor(out=fours, in0=fours, in1=loop_cap[:].rearrange("p (m q) -> p m q", q=SLOTS), op=ALU.min)

        def square(engine, g, c, s):
            src = root[g, c][:].rearrange("p (a m s e) -> p s m a e", a=2, s=SLOTS, e=2)[:, s]
            dst = adj[g, c][:, s * PASS:(s + 1) * PASS].rearrange("p (m a e) -> p m a e", a=2, e=2)
            if engine == SCALAR:
                nc.scalar.activation(out=dst, in_=src, func=ACT.Square)
            else:
                nc.vector.tensor_tensor(out=dst, in0=src, in1=src, op=ALU.mult)

        def quantise(values, codes, scales, fmt, first, count):
            nc.vector.quantize_mx(out=codes[:, first:first + count].bitcast(fmt), scales=scales[:, first:first + count],
                                  in_=values)

        def quantise_adj(g, c, s_first, s_end):
            quantise(adj[g, c][:, s_first * PASS:s_end * PASS], adj_codes[g, c], adj_scales[g, c], E4M3,
                     s_first * P, (s_end - s_first) * P)

        def gate_rows(g, pair):
            for e in range(2):
                t = 2 * pair + e
                nc.vector.tensor_scalar(out=gate[g][:, t * H:(t + 1) * H], in0=z_rows[g, pair][:, e * H:(e + 1) * H],
                                        scalar1=0.0, scalar2=dinv[:, g * SLOTS + t:g * SLOTS + t + 1],
                                        op0=ALU.is_gt, op1=ALU.mult)

        def round_dz2(g, half):
            order = "p (t k c i) -> p k c t i"
            dst = dz2[g][:, half * 2 * H:(half + 1) * 2 * H].rearrange("p (c i t) -> p c t i", i=2, t=SLOTS)
            nc.vector.tensor_tensor(out=dst, in0=gate[g][:].rearrange(order, t=SLOTS, k=2, i=2)[:, half],
                                    in1=grad[g][:].rearrange(order, t=SLOTS, k=2, i=2)[:, half], op=ALU.mult)

        def quantise_dz2(g):
            quantise(dz2[g][:], dz2_codes[g], dz2_scales[g], E5M2, 0, H)

        def dh_pass(g, c, s):
            if g == 0:
                dh[c, s] = bank(SLOTS * c + s, "dh%d%d" % (c, s))
            cols = slice(s * P, (s + 1) * P)
            nc.tensor.matmul_mx(out=dh[c, s][:], lhsT=adj_codes[g, c][:, cols].bitcast(E4M3), lhsT_scale=adj_scales[g, c][:, cols],
                                rhs=dz2_codes[g][:].bitcast(E5M2), rhs_scale=dz2_scales[g][:],
                                start=(g == 0), stop=(g == PASSES - 1))

        def round_dz1(engine, c, s):
            src = dh[c, s][:].rearrange("p (w u e) -> p u w e", u=2, e=2)
            dst = dz1_rows[c][:, s * H:(s + 1) * H].rearrange("p (u w e) -> p u w e", u=2, e=2)
            factor = dinv[:, c * SLOTS + s:c * SLOTS + s + 1]
            if engine == SCALAR:
                nc.scalar.activation(out=dst, in_=src, func=ACT.Copy, scale=factor)
            else:
                nc.vector.tensor_scalar(out=dst, in0=src, scalar1=factor, scalar2=None, op0=ALU.mult)

        def flip_dz1(c, pair):
            flipped[c, pair] = bank(SLOTS * c + 2 * pair, "flipped%d%d" % (c, pair))
            words = dz1_rows[c][:, pair * 2 * H:(pair + 1) * 2 * H].bitcast(F32)
            for block in range(SLOTS):
                cols = slice(block * P, (block + 1) * P)
                nc.tensor.transpose(flipped[c, pair][:, cols], words[:, cols], ident[:])

        def copy(engine, dst, src):
            if engine == SCALAR:
                nc.scalar.copy(out=dst, in_=src)
            else:
                nc.vector.tensor_copy(out=dst, in_=src)

        def pack_feat(c, pair):
            copy(SCALAR, dz1_by_feat[c, pair][:].bitcast(F32).rearrange("p (e m u) -> p e m u", e=2, u=2),
                 flipped[c, pair][:].rearrange("p (e u m) -> p e m u", e=2, u=2))

        def quantise_feat(c, pair):
            quantise(dz1_by_feat[c, pair][:], feat_codes[c, pair], feat_scales[c, pair], E5M2, 0, 2 * P)

        def dx_passes(c, pair):
            dx_sum[c, pair] = bank(SLOTS * c + 2 * pair + 1, "dx_sum%d%d" % (c, pair))
            for e in range(2):
                cols = slice(e * P, (e + 1) * P)
                window = slice((1 - e) * D, (1 - e) * D + PASS)
                nc.tensor.matmul_mx(out=dx_sum[c, pair][:], lhsT=feat_codes[c, pair][:, cols].bitcast(E5M2),
                                    lhsT_scale=feat_scales[c, pair][:, cols],
                                    rhs=w_codes[:, window].bitcast(E4M3), rhs_scale=w_scales[:, window],
                                    start=(e == 0), stop=(e == 1))

        def store_dx(c, pair):
            copy(SCALAR, dx_rows[c, pair][:], dx_sum[c, pair][:, 0:2 * D])
            nc.sync.dma_start(out=pair_of_rows(out_0, c, pair), in_=dx_rows[c, pair][:].rearrange("p (e d) -> p e d", e=2))

        def pack_node(c, half):
            src = dz1_rows[c][:].rearrange("p (s k n i) -> p k n s i", s=SLOTS, k=2, i=4)[:, half]
            dst = dz1_by_node[c][:, half * 2 * H:(half + 1) * 2 * H].rearrange("p (n i s) -> p n s i", i=4, s=SLOTS)
            nc.vector.tensor_copy(out=dst, in_=src)

        def quantise_node(c, half):
            quantise(dz1_by_node[c][:, half * 2 * H:(half + 1) * 2 * H], node_codes[c], node_scales[c], E5M2,
                     half * H // 2, H // 2)

        def dw_pass(c, first):
            if first:
                single["dw"] = bank(SLOTS * c, "dw_sum")
            cols = slice(c * D, (c + 1) * D)
            nc.tensor.matmul_mx(out=single["dw"][:], lhsT=x_codes[:, cols].bitcast(E4M3), lhsT_scale=x_scales[:, cols],
                                rhs=node_codes[c][:].bitcast(E5M2), rhs_scale=node_scales[c][:],
                                start=first, stop=not first)

        def store_dw():
            copy(VECTOR, dw_rows[:].rearrange("p (w u e) -> p w u e", u=2, e=2),
                 single["dw"][:].rearrange("p (u w e) -> p w u e", u=2, e=2))
            nc.sync.dma_start(out=out_1, in_=dw_rows[:])

        def pack_x():
            nc.vector.tensor_copy(out=x_packed[:].rearrange("p (c n i s) -> p c n s i", c=PASSES, i=4, s=SLOTS),
                                  in_=x_rows[:].rearrange("p (c s n i) -> p c n s i", c=PASSES, s=SLOTS, i=4))

        def quantise_x():
            quantise(x_packed[:], x_codes, x_scales, E4M3, 0, PASSES * D)

        def flip_w():
            single["w"] = bank(SLOTS + 2, "flipped_w")
            words = w_rows[:].bitcast(F32)
            for u in range(2):
                nc.tensor.transpose(single["w"][:, u * P:(u + 1) * P], words[:, u:2 * P:2], ident[:])

        def pack_w():
            copy(VECTOR, w_packed[:].bitcast(F32).rearrange("p (d u) -> p d u", u=2),
                 single["w"][:, 0:2 * P].rearrange("p (u d) -> p d u", u=2))

        def quantise_w():
            quantise(w_packed[:], w_codes, w_scales, E4M3, D, D)

        load_dist(0, 0, 0)
        constants()
        load_dist(0, 0, 1)
        load_dinv()
        load_dist(1, 1, 0)
        for pair in range(2):
            load_z(0, pair)
        for pair in range(2):
            load_dist(0, 1, pair)
        load_grad(0)
        load_dist(1, 1, 1)
        for pair in range(2):
            load_z(1, pair)
        load_w()
        load_grad(1)
        for pair in range(2):
            load_dist(1, 0, pair)
        load_x()

        for pair in range(2):
            inverse_root(0, 0, pair)
        inverse_root(1, 1, 0)
        for pair in range(2):
            self_loops(0, pair)
        for pair in range(2):
            gate_rows(0, pair)
            square(SCALAR, 0, 0, pair)
            square(VECTOR, 0, 0, 2 + pair)
        self_loops(1, 0)
        quantise_adj(0, 0, 0, SLOTS)

        for pair in range(2):
            inverse_root(0, 1, pair)
        inverse_root(1, 1, 1)
        for s in range(SLOTS):
            square(SCALAR, 0, 1, s)
        for half in range(2):
            round_dz2(0, half)
        self_loops(1, 1)
        quantise_dz2(0)
        for pair in range(2):
            gate_rows(1, pair)
        quantise_adj(0, 1, 0, SLOTS)
        for s in range(SLOTS):
            square(SCALAR, 1, 1, s)
        flip_w()
        for s in range(SLOTS):
            dh_pass(0, 0, s)
        for half in range(2):
            round_dz2(1, half)
        pack_w()
        quantise_dz2(1)
        quantise_adj(1, 1, 0, SLOTS)
        for g in range(PASSES):
            for s in range(SLOTS):
                dh_pass(g, 1, s)

        for pair in range(2):
            inverse_root(1, 0, pair)
        for s in (0, 1, 3):
            square(SCALAR, 1, 0, s)
        pack_x()
        square(VECTOR, 1, 0, 2)
        quantise_w()
        quantise_x()
        quantise_adj(1, 0, 0, 2)
        round_dz1(VECTOR, 1, 0)
        quantise_adj(1, 0, 2, SLOTS)
        for s in range(1, SLOTS - 1):
            round_dz1(SCALAR, 1, s)
        round_dz1(VECTOR, 1, SLOTS - 1)
        for pair in range(2):
            for s in range(2 * pair, 2 * pair + 2):
                dh_pass(1, 0, s)
            flip_dz1(1, pair)

        for s in range(2):
            round_dz1(SCALAR, 0, s)
        pack_feat(1, 0)
        for s in range(2, SLOTS):
            round_dz1(SCALAR, 0, s)
        for half in range(2):
            pack_node(1, half)
        quantise_feat(1, 0)
        for half in range(2):
            quantise_node(1, half)
        flip_dz1(0, 0)
        dx_passes(1, 0)
        flip_dz1(0, 1)
        dw_pass(1, True)
        pack_feat(0, 0)
        pack_feat(1, 1)
        pack_feat(0, 1)
        pack_node(0, 0)
        quantise_feat(0, 0)
        pack_node(0, 1)
        quantise_feat(1, 1)
        for half in range(2):
            quantise_node(0, half)
        quantise_feat(0, 1)
        dx_passes(0, 0)
        dx_passes(1, 1)
        dw_pass(0, False)
        dx_passes(0, 1)

        store_dx(1, 0)
        store_dx(0, 0)
        store_dx(1, 1)
        store_dw()
        store_dx(0, 1)
